import numpy as np
import ml_dtypes


def mxq(x, axis, fmt="e4m3"):
    dtype, down = {"e4m3": (ml_dtypes.float8_e4m3fn, 7), "e5m2": (ml_dtypes.float8_e5m2, 14)}[fmt]
    v = np.moveaxis(np.asarray(x, np.float32).astype(ml_dtypes.bfloat16).astype(np.float64), axis, -1)
    blocks = v.reshape(v.shape[:-1] + (-1, 32))
    amax = np.abs(blocks).max(-1, keepdims=True)
    byte = np.maximum(np.where(amax > 0, np.frexp(amax)[1] - 1 + 127, 0) - down, 1)
    scale = np.exp2(byte - 127.0)
    codes = (blocks / scale).astype(np.float32).astype(dtype).astype(np.float64)
    return np.moveaxis((codes * scale).reshape(v.shape), -1, axis)


WIDE = False


def mx_kscale(k):
    if not WIDE:
        return np.ones(k)
    levels = np.array([10, -10, 5, -5, 0])
    a = np.random.permutation(np.resize(levels, k // 512 * 4)).reshape(k // 512, 4)
    idx = np.arange(k)
    return np.exp2(a[idx // 512, idx % 128 // 32])


BF16 = ml_dtypes.bfloat16


def bf(x):
    return np.asarray(x, np.float32).astype(BF16)


def f64(x):
    return np.asarray(x).astype(np.float64)


E2M1 = np.array([0.0, 0.5, 1.0, 1.5, 2.0, 3.0, 4.0, 6.0, -0.0, -0.5, -1.0, -1.5, -2.0, -3.0, -4.0, -6.0])


def pack_weight(w, fmt):
    k, n = w.shape
    w = f64(bf(w)).reshape(k // 32, 32, n)
    amax = np.abs(w).max(1)
    if fmt == "e4m3":
        byte = np.frexp(amax)[1] - 1 + 127 - 7
    else:
        mant, ex = np.frexp(amax / 6.0)
        byte = np.where(mant > 0.5, ex, ex - 1) + 127
    byte = np.clip(np.where(amax > 0, byte, 1), 1, 254)
    scaled = (w * np.exp2(127.0 - byte)[:, None, :]).reshape(k, n).astype(np.float32)
    by_word = np.ascontiguousarray(scaled.reshape(k // 512, 128, 4, n).transpose(0, 1, 3, 2))
    if fmt == "e4m3":
        words = by_word.astype(ml_dtypes.float8_e4m3fn).view(np.uint8)
    else:
        c = by_word.astype(ml_dtypes.float4_e2m1fn).view(np.uint8) & 0xF
        words = c[..., 0::2] | (c[..., 1::2] << 4)
    return np.ascontiguousarray(words), np.ascontiguousarray(byte.astype(np.uint8).reshape(k // 512, 16, n))


def unpack_weight(words, scales, fmt):
    g, p, n, _ = words.shape
    if fmt == "e4m3":
        vals = np.ascontiguousarray(words).view(ml_dtypes.float8_e4m3fn).astype(np.float64)
    else:
        nib = np.empty((g, p, n, 4), np.uint8)
        nib[..., 0::2] = words & 0xF
        nib[..., 1::2] = words >> 4
        vals = E2M1[nib]
    vals = vals * np.repeat(np.exp2(scales.astype(np.float64) - 127.0), 8, axis=1)[..., None]
    return vals.transpose(0, 1, 3, 2).reshape(g * 512, n)

def pack4(w):
    words, scales = pack_weight(w, "e2m1")
    return words.reshape(words.shape[0], 128, -1), scales


def unpack4(words, scales):
    return unpack_weight(words.reshape(words.shape[0], 128, -1, 2), scales, "e2m1")


T, DIM, H, HKV, D = 128, 512, 16, 4, 128
THETA = 10000.0
NQ, NK = H * D, HKV * D


def rope(u):
    inv_freq = 1.0 / THETA ** (np.arange(0, D, 2) / D)
    ang = np.arange(T)[:, None] * inv_freq
    cos, sin = np.cos(ang)[:, None, :], np.sin(ang)[:, None, :]
    p = u.reshape(T, -1, D // 2, 2)
    u1, u2 = p[..., 0], p[..., 1]
    return np.stack([u1 * cos - u2 * sin, u1 * sin + u2 * cos], axis=-1).reshape(u.shape)


def setup_inputs():
    s = mx_kscale(DIM)
    x = bf(np.random.standard_normal((T, DIM)) * s)
    words, scales = pack4((np.random.standard_normal((NQ + NK + NK, DIM)) / np.sqrt(DIM) / s).T)
    return {"x": x, "w_qkv_words": words, "w_qkv_scales": scales}


def reference(x, w_qkv_words, w_qkv_scales):
    qkv = mxq(f64(x), 1, "e4m3") @ unpack4(w_qkv_words, w_qkv_scales)
    q = qkv[:, :NQ].reshape(T, H, D)
    k = qkv[:, NQ:NQ + NK].reshape(T, HKV, D)
    v = qkv[:, NQ + NK:].reshape(T, HKV, D)
    return rope(q), rope(k), v

@@ -1,0 +1,175 @@
+import math
+
+import concourse.mybir as mybir
+from concourse.masks import make_identity
+
+F32 = mybir.dt.float32
+BF16 = mybir.dt.bfloat16
+I32 = mybir.dt.int32
+U32 = mybir.dt.uint32
+U8 = mybir.dt.uint8
+FP8X4 = mybir.dt.float8_e4m3fn_x4
+FP4X4 = mybir.dt.float4_e2m1fn_x4
+ALU = mybir.AluOpType
+ACT = mybir.ActivationFunctionType
+
+P = 128
+DIM = 512
+HEAD = 128
+PAIRS = HEAD // 2
+Q_HEADS, KV_HEADS = 16, 4
+N_ALL = (Q_HEADS + 2 * KV_HEADS) * HEAD
+BANK = 512
+HEADS_PER_BANK = BANK // HEAD
+ROPE_BANKS = (Q_HEADS + KV_HEADS) // HEADS_PER_BANK
+W_LOADS = 3
+THETA = 10000.0
+TWO_PI = 2.0 * math.pi
+
+FLOPS = 2 * P * DIM * N_ALL
+
+
+def tile_attention_pa_s_kernel(tc, x, w_qkv_words, w_qkv_scales, out_0, out_1, out_2):
+    nc = tc.nc
+    with tc.tile_pool(name="keep", bufs=1) as keep, tc.tile_pool(name="work", bufs=ROPE_BANKS) as work, tc.psum_pool(
+        name="psum", bufs=1
+    ) as psum:
+        x_sb = keep.tile([P, DIM], BF16)
+        nc.sync.dma_start(out=x_sb[:], in_=x)
+
+        w_scales = keep.tile([P, N_ALL], U8, align_bytes=64)
+        nc.vector.memset(w_scales[:].bitcast(I32), 0)
+        for quadrant in range(4):
+            nc.sync.dma_start(
+                out=w_scales[32 * quadrant : 32 * quadrant + 4, :].bitcast(I32),
+                in_=w_qkv_scales[0, 4 * quadrant : 4 * quadrant + 4, :].bitcast(I32),
+            )
+
+        w_words = keep.tile([P, 2 * N_ALL], U8, align_bytes=64)
+        load_bytes = 2 * N_ALL // W_LOADS
+        for c in range(W_LOADS):
+            cols = slice(c * load_bytes, (c + 1) * load_bytes)
+            nc.sync.dma_start(out=w_words[:, cols].bitcast(I32), in_=w_qkv_words[0, :, cols].bitcast(I32))
+
+        token = keep.tile([P, 1], F32)
+        nc.gpsimd.iota(token[:], pattern=[[0, 1]], base=0, channel_multiplier=1, allow_small_or_imprecise_dtypes=True)
+        ident = keep.tile([P, P], F32)
+        make_identity(nc, ident[:])
+
+        freq = keep.tile([P, PAIRS], F32)
+        nc.vector.memset(freq[:, 0:1], 1.0)
+        width = 1
+        while width < PAIRS:
+            nc.vector.tensor_scalar(
+                out=freq[:, width : 2 * width],
+                in0=freq[:, 0:width],
+                scalar1=THETA ** (-width / PAIRS),
+                scalar2=None,
+                op0=ALU.mult,
+            )
+            width *= 2
+        token_turns = keep.tile([P, 1], F32)
+        nc.vector.tensor_scalar(out=token_turns[:], in0=token[:], scalar1=1.0 / TWO_PI, scalar2=None, op0=ALU.mult)
+        turns = keep.tile([P, 2, PAIRS], F32)
+        for part, shift in enumerate((0.25, 0.0)):
+            nc.vector.tensor_scalar(
+                out=turns[:, part, :],
+                in0=freq[:],
+                scalar1=token_turns[:, 0:1],
+                scalar2=shift,
+                op0=ALU.mult,
+                op1=ALU.add,
+            )
+        whole = keep.tile([P, 2, PAIRS], I32)
+        nc.vector.tensor_copy(out=whole[:], in_=turns[:])
+        left = keep.tile([P, 2, PAIRS], F32)
+        nc.vector.tensor_tensor(out=left[:], in0=turns[:], in1=whole[:], op=ALU.subtract)
+        minus_turns = keep.tile([P, 2, PAIRS], F32)
+        nc.vector.scalar_tensor_tensor(
+            out=minus_turns[:].rearrange("p a i -> p (a i)"),
+            in0=left[:].rearrange("p a i -> p (a i)"),
+            scalar=0.5,
+            in1=left[:].rearrange("p a i -> p (a i)"),
+            op0=ALU.is_gt,
+            op1=ALU.subtract,
+        )
+        cos_twice = keep.tile([P, PAIRS, 2], F32)
+        nc.scalar.activation(
+            out=cos_twice[:],
+            in_=minus_turns[:, 0, :].unsqueeze(2).to_broadcast([P, PAIRS, 2]),
+            func=ACT.Sin,
+            scale=-TWO_PI,
+        )
+        sin_plus = keep.tile([P, PAIRS], F32)
+        nc.scalar.activation(out=sin_plus[:], in_=minus_turns[:, 1, :], func=ACT.Sin, scale=-TWO_PI)
+        sin_minus = keep.tile([P, PAIRS], F32)
+        nc.scalar.activation(out=sin_minus[:], in_=minus_turns[:, 1, :], func=ACT.Sin, scale=TWO_PI)
+
+        x_words = x_sb[:].bitcast(F32)
+        x_t = psum.tile([P, 2, P], F32)
+        for u in range(2):
+            nc.tensor.transpose(x_t[:, u, :], x_words[:, u : DIM // 2 : 2], ident[:])
+        x_grouped = keep.tile([P, 4 * P], BF16, align_bytes=64)
+        nc.vector.tensor_copy(
+            out=x_grouped[:].bitcast(F32).rearrange("p (t u) -> p t u", u=2),
+            in_=x_t[:].rearrange("p u t -> p t u"),
+        )
+        x_codes = keep.tile([P, P], U32, align_bytes=64)
+        x_scales = keep.tile([P, P], U8, align_bytes=64)
+        nc.vector.quantize_mx(out=x_codes[:].bitcast(FP8X4), scales=x_scales[:], in_=x_grouped[:])
+
+        banks = []
+        for b in range(N_ALL // BANK):
+            acc = psum.tile([P, BANK], F32, name="acc%d" % b)
+            nc.tensor.matmul_mx(
+                out=acc[:],
+                lhsT=x_codes[:].bitcast(FP8X4),
+                lhsT_scale=x_scales[:],
+                rhs=w_words[:, 2 * BANK * b : 2 * BANK * (b + 1)].bitcast(FP4X4),
+                rhs_scale=w_scales[:, BANK * b : BANK * (b + 1)],
+                start=True,
+                stop=True,
+            )
+            banks.append(acc)
+
+        v_sb = keep.tile([P, BANK], F32)
+        nc.scalar.copy(out=v_sb[:], in_=banks[ROPE_BANKS][:])
+        nc.scalar.dma_start(out=out_2.rearrange("t n d -> t (n d)"), in_=v_sb[:])
+
+        q_flat = out_0.rearrange("t n d -> t (n d)")
+        k_flat = out_1.rearrange("t n d -> t (n d)")
+        for b in range(ROPE_BANKS):
+            u_heads = banks[b][:].rearrange("p (n c) -> p n c", n=HEADS_PER_BANK)
+            u_pairs = banks[b][:].rearrange("p (n i h) -> p n i h", n=HEADS_PER_BANK, h=2)
+            own = work.tile([P, HEADS_PER_BANK, HEAD], F32)
+            nc.vector.tensor_tensor(
+                out=own[:],
+                in0=u_heads,
+                in1=cos_twice[:].rearrange("p i h -> p (i h)").unsqueeze(1).to_broadcast([P, HEADS_PER_BANK, HEAD]),
+                op=ALU.mult,
+            )
+            other = work.tile([P, 2, HEADS_PER_BANK, PAIRS], F32)
+            nc.vector.tensor_tensor(
+                out=other[:, 0],
+                in0=u_pairs[:, :, :, 1],
+                in1=sin_minus[:].unsqueeze(1).to_broadcast([P, HEADS_PER_BANK, PAIRS]),
+                op=ALU.mult,
+            )
+            nc.vector.tensor_tensor(
+                out=other[:, 1],
+                in0=u_pairs[:, :, :, 0],
+                in1=sin_plus[:].unsqueeze(1).to_broadcast([P, HEADS_PER_BANK, PAIRS]),
+                op=ALU.mult,
+            )
+            adder = nc.vector if b == ROPE_BANKS - 1 else nc.gpsimd
+            rotated = work.tile([P, BANK], F32)
+            adder.tensor_tensor(
+                out=rotated[:].rearrange("p (c h) -> p c h", h=2),
+                in0=own[:].rearrange("p n (i h) -> p (n i) h", h=2),
+                in1=other[:].rearrange("p h n i -> p (n i) h"),
+                op=ALU.add,
+            )
+            if b < Q_HEADS // HEADS_PER_BANK:
+                nc.sync.dma_start(out=q_flat[:, BANK * b : BANK * (b + 1)], in_=rotated[:])
+            else:
+                nc.sync.dma_start(out=k_flat, in_=rotated[:])

@@ -22,7 +22,6 @@ N_ALL = (Q_HEADS + 2 * KV_HEADS) * HEAD
 BANK = 512
 HEADS_PER_BANK = BANK // HEAD
 ROPE_BANKS = (Q_HEADS + KV_HEADS) // HEADS_PER_BANK
-W_LOADS = 3
 THETA = 10000.0
 TWO_PI = 2.0 * math.pi
 
@@ -33,90 +32,91 @@ def tile_attention_pa_s_kernel(tc, x, w_qkv_words, w_qkv_scales, out_0, out_1, o
     nc = tc.nc
     with tc.tile_pool(name="keep", bufs=1) as keep, tc.tile_pool(name="work", bufs=ROPE_BANKS) as work, tc.psum_pool(
         name="psum", bufs=1
-    ) as psum:
+    ) as psum, tc.manual_schedule():
         x_sb = keep.tile([P, DIM], BF16)
         nc.sync.dma_start(out=x_sb[:], in_=x)
 
+        w_words = keep.tile([P, 2 * N_ALL], U8, align_bytes=64)
+
+        def load_words(first_bank, n_banks):
+            cols = slice(2 * BANK * first_bank, 2 * BANK * (first_bank + n_banks))
+            nc.sync.dma_start(out=w_words[:, cols].bitcast(I32), in_=w_qkv_words[0, :, cols].bitcast(I32))
+
         w_scales = keep.tile([P, N_ALL], U8, align_bytes=64)
         nc.vector.memset(w_scales[:].bitcast(I32), 0)
+
+        load_words(0, 1)
         for quadrant in range(4):
             nc.sync.dma_start(
                 out=w_scales[32 * quadrant : 32 * quadrant + 4, :].bitcast(I32),
                 in_=w_qkv_scales[0, 4 * quadrant : 4 * quadrant + 4, :].bitcast(I32),
             )
-
-        w_words = keep.tile([P, 2 * N_ALL], U8, align_bytes=64)
-        load_bytes = 2 * N_ALL // W_LOADS
-        for c in range(W_LOADS):
-            cols = slice(c * load_bytes, (c + 1) * load_bytes)
-            nc.sync.dma_start(out=w_words[:, cols].bitcast(I32), in_=w_qkv_words[0, :, cols].bitcast(I32))
+        load_words(1, 2)
+        load_words(3, 3)
 
         token = keep.tile([P, 1], F32)
         nc.gpsimd.iota(token[:], pattern=[[0, 1]], base=0, channel_multiplier=1, allow_small_or_imprecise_dtypes=True)
+        token_turns = keep.tile([P, 1], F32)
+        nc.gpsimd.tensor_scalar(
+            out=token_turns[:], in0=token[:], scalar1=1.0 / TWO_PI, scalar2=0.0, op0=ALU.mult, op1=ALU.add
+        )
         ident = keep.tile([P, P], F32)
         make_identity(nc, ident[:])
+        shift = keep.tile([P, 3], F32)
+        nc.gpsimd.memset(shift[:], 0.0)
+        nc.gpsimd.memset(shift[:, 0:1], 0.25)
 
-        freq = keep.tile([P, PAIRS], F32)
-        nc.vector.memset(freq[:, 0:1], 1.0)
-        width = 1
-        while width < PAIRS:
-            nc.vector.tensor_scalar(
-                out=freq[:, width : 2 * width],
-                in0=freq[:, 0:width],
-                scalar1=THETA ** (-width / PAIRS),
-                scalar2=None,
-                op0=ALU.mult,
-            )
-            width *= 2
-        token_turns = keep.tile([P, 1], F32)
-        nc.vector.tensor_scalar(out=token_turns[:], in0=token[:], scalar1=1.0 / TWO_PI, scalar2=None, op0=ALU.mult)
-        turns = keep.tile([P, 2, PAIRS], F32)
-        for part, shift in enumerate((0.25, 0.0)):
-            nc.vector.tensor_scalar(
-                out=turns[:, part, :],
+        freq = keep.tile([P, 3, PAIRS], F32)
+        nc.vector.memset(freq[:, :, 0:1], 1.0)
+        nc.vector.memset(freq[:, 1, 0:1], -1.0)
+        sin_first = keep.tile([P, 1], F32)
+        nc.scalar.activation(out=sin_first[:], in_=freq[:, 0, 0:1], func=ACT.Sin)
+        for level in (1, 4, 16):
+            for m in (1, 2, 3):
+                nc.vector.tensor_scalar(
+                    out=freq[:, :, m * level : (m + 1) * level],
+                    in0=freq[:, :, 0:level],
+                    scalar1=THETA ** (-m * level / PAIRS),
+                    scalar2=None,
+                    op0=ALU.mult,
+                )
+        shift_wide = shift[:].unsqueeze(2).to_broadcast([P, 3, PAIRS])
+        turns = keep.tile([P, 3, PAIRS], F32)
+        whole = keep.tile([P, 3, PAIRS], I32)
+        for rounded_or_not in (turns, whole):
+            nc.vector.scalar_tensor_tensor(
+                out=rounded_or_not[:],
                 in0=freq[:],
-                scalar1=token_turns[:, 0:1],
-                scalar2=shift,
+                scalar=token_turns[:, 0:1],
+                in1=shift_wide,
                 op0=ALU.mult,
                 op1=ALU.add,
             )
-        whole = keep.tile([P, 2, PAIRS], I32)
-        nc.vector.tensor_copy(out=whole[:], in_=turns[:])
-        left = keep.tile([P, 2, PAIRS], F32)
+        left = keep.tile([P, 3, PAIRS], F32)
         nc.vector.tensor_tensor(out=left[:], in0=turns[:], in1=whole[:], op=ALU.subtract)
-        minus_turns = keep.tile([P, 2, PAIRS], F32)
-        nc.vector.scalar_tensor_tensor(
-            out=minus_turns[:].rearrange("p a i -> p (a i)"),
-            in0=left[:].rearrange("p a i -> p (a i)"),
-            scalar=0.5,
-            in1=left[:].rearrange("p a i -> p (a i)"),
-            op0=ALU.is_gt,
-            op1=ALU.subtract,
-        )
-        cos_twice = keep.tile([P, PAIRS, 2], F32)
-        nc.scalar.activation(
-            out=cos_twice[:],
-            in_=minus_turns[:, 0, :].unsqueeze(2).to_broadcast([P, PAIRS, 2]),
-            func=ACT.Sin,
-            scale=-TWO_PI,
-        )
-        sin_plus = keep.tile([P, PAIRS], F32)
-        nc.scalar.activation(out=sin_plus[:], in_=minus_turns[:, 1, :], func=ACT.Sin, scale=-TWO_PI)
-        sin_minus = keep.tile([P, PAIRS], F32)
-        nc.scalar.activation(out=sin_minus[:], in_=minus_turns[:, 1, :], func=ACT.Sin, scale=TWO_PI)
 
         x_words = x_sb[:].bitcast(F32)
         x_t = psum.tile([P, 2, P], F32)
         for u in range(2):
             nc.tensor.transpose(x_t[:, u, :], x_words[:, u : DIM // 2 : 2], ident[:])
         x_grouped = keep.tile([P, 4 * P], BF16, align_bytes=64)
-        nc.vector.tensor_copy(
+        nc.scalar.copy(
             out=x_grouped[:].bitcast(F32).rearrange("p (t u) -> p t u", u=2),
             in_=x_t[:].rearrange("p u t -> p t u"),
         )
         x_codes = keep.tile([P, P], U32, align_bytes=64)
         x_scales = keep.tile([P, P], U8, align_bytes=64)
         nc.vector.quantize_mx(out=x_codes[:].bitcast(FP8X4), scales=x_scales[:], in_=x_grouped[:])
+
+        cos_twice = keep.tile([P, PAIRS, 2], F32)
+        nc.scalar.activation(
+            out=cos_twice[:],
+            in_=left[:, 0, :].unsqueeze(2).to_broadcast([P, PAIRS, 2]),
+            func=ACT.Sin,
+            scale=TWO_PI,
+        )
+        sines = keep.tile([P, 2, PAIRS], F32)
+        nc.scalar.activation(out=sines[:], in_=left[:, 1:3, :], func=ACT.Sin, scale=TWO_PI)
 
         banks = []
         for b in range(N_ALL // BANK):
@@ -149,27 +149,28 @@ def tile_attention_pa_s_kernel(tc, x, w_qkv_words, w_qkv_scales, out_0, out_1, o
                 op=ALU.mult,
             )
             other = work.tile([P, 2, HEADS_PER_BANK, PAIRS], F32)
-            nc.vector.tensor_tensor(
-                out=other[:, 0],
-                in0=u_pairs[:, :, :, 1],
-                in1=sin_minus[:].unsqueeze(1).to_broadcast([P, HEADS_PER_BANK, PAIRS]),
-                op=ALU.mult,
-            )
-            nc.vector.tensor_tensor(
-                out=other[:, 1],
-                in0=u_pairs[:, :, :, 0],
-                in1=sin_plus[:].unsqueeze(1).to_broadcast([P, HEADS_PER_BANK, PAIRS]),
-                op=ALU.mult,
-            )
-            adder = nc.vector if b == ROPE_BANKS - 1 else nc.gpsimd
-            rotated = work.tile([P, BANK], F32)
-            adder.tensor_tensor(
-                out=rotated[:].rearrange("p (c h) -> p c h", h=2),
-                in0=own[:].rearrange("p n (i h) -> p (n i) h", h=2),
-                in1=other[:].rearrange("p h n i -> p (n i) h"),
-                op=ALU.add,
-            )
-            if b < Q_HEADS // HEADS_PER_BANK:
-                nc.sync.dma_start(out=q_flat[:, BANK * b : BANK * (b + 1)], in_=rotated[:])
-            else:
-                nc.sync.dma_start(out=k_flat, in_=rotated[:])
+            for h in range(2):
+                nc.vector.tensor_tensor(
+                    out=other[:, h],
+                    in0=u_pairs[:, :, :, 1 - h],
+                    in1=sines[:, h, :].unsqueeze(1).to_broadcast([P, HEADS_PER_BANK, PAIRS]),
+                    op=ALU.mult,
+                )
+            last = b == ROPE_BANKS - 1
+            adder = nc.vector if last else nc.gpsimd
+            pieces = 2 if last else 1
+            dest = q_flat[:, BANK * b : BANK * (b + 1)] if b < Q_HEADS // HEADS_PER_BANK else k_flat
+            rotated = work.tile([P, HEADS_PER_BANK, HEAD], F32)
+            heads = HEADS_PER_BANK // pieces
+            for piece in range(pieces):
+                n = slice(piece * heads, (piece + 1) * heads)
+                adder.tensor_tensor(
+                    out=rotated[:, n, :].rearrange("p n (i h) -> p (n i) h", h=2),
+                    in0=own[:, n, :].rearrange("p n (i h) -> p (n i) h", h=2),
+                    in1=other[:, :, n, :].rearrange("p h n i -> p (n i) h"),
+                    op=ALU.add,
+                )
+                nc.sync.dma_start(
+                    out=dest[:, HEAD * heads * piece : HEAD * heads * (piece + 1)],
+                    in_=rotated[:, n, :].rearrange("p n c -> p (n c)"),
+                )

@@ -24,6 +24,7 @@ HEADS_PER_BANK = BANK // HEAD
 ROPE_BANKS = (Q_HEADS + KV_HEADS) // HEADS_PER_BANK
 THETA = 10000.0
 TWO_PI = 2.0 * math.pi
+WARM_MATMULS = 4
 
 FLOPS = 2 * P * DIM * N_ALL
 
@@ -54,6 +55,8 @@ def tile_attention_pa_s_kernel(tc, x, w_qkv_words, w_qkv_scales, out_0, out_1, o
         load_words(1, 2)
         load_words(3, 3)
 
+        warm = keep.tile([P, P], F32)
+        nc.gpsimd.memset(warm[:], 0.0)
         token = keep.tile([P, 1], F32)
         nc.gpsimd.iota(token[:], pattern=[[0, 1]], base=0, channel_multiplier=1, allow_small_or_imprecise_dtypes=True)
         token_turns = keep.tile([P, 1], F32)
@@ -95,6 +98,9 @@ def tile_attention_pa_s_kernel(tc, x, w_qkv_words, w_qkv_scales, out_0, out_1, o
         left = keep.tile([P, 3, PAIRS], F32)
         nc.vector.tensor_tensor(out=left[:], in0=turns[:], in1=whole[:], op=ALU.subtract)
 
+        warm_out = psum.tile([P, P], F32)
+        for i_warm in range(WARM_MATMULS):
+            nc.tensor.matmul(warm_out[:], lhsT=warm[:], rhs=warm[:], start=True, stop=True)
         x_words = x_sb[:].bitcast(F32)
         x_t = psum.tile([P, 2, P], F32)
         for u in range(2):

@@ -25,6 +25,7 @@ ROPE_BANKS = (Q_HEADS + KV_HEADS) // HEADS_PER_BANK
 THETA = 10000.0
 TWO_PI = 2.0 * math.pi
 WARM_MATMULS = 4
+GPSIMD_SUMS = 3
 
 FLOPS = 2 * P * DIM * N_ALL
 
@@ -144,6 +145,26 @@ def tile_attention_pa_s_kernel(tc, x, w_qkv_words, w_qkv_scales, out_0, out_1, o
 
         q_flat = out_0.rearrange("t n d -> t (n d)")
         k_flat = out_1.rearrange("t n d -> t (n d)")
+        products = []
+
+        def add_and_store(adder, b, pieces):
+            own, other = products[b]
+            dest = q_flat[:, BANK * b : BANK * (b + 1)] if b < Q_HEADS // HEADS_PER_BANK else k_flat
+            rotated = work.tile([P, HEADS_PER_BANK, HEAD], F32, name="rotated")
+            heads = HEADS_PER_BANK // pieces
+            for piece in range(pieces):
+                n = slice(piece * heads, (piece + 1) * heads)
+                adder.tensor_tensor(
+                    out=rotated[:, n, :].rearrange("p n (i h) -> p (n i) h", h=2),
+                    in0=own[:, n, :].rearrange("p n (i h) -> p (n i) h", h=2),
+                    in1=other[:, :, n, :].rearrange("p h n i -> p (n i) h"),
+                    op=ALU.add,
+                )
+                nc.sync.dma_start(
+                    out=dest[:, HEAD * heads * piece : HEAD * heads * (piece + 1)],
+                    in_=rotated[:, n, :].rearrange("p n c -> p (n c)"),
+                )
+
         for b in range(ROPE_BANKS):
             u_heads = banks[b][:].rearrange("p (n c) -> p n c", n=HEADS_PER_BANK)
             u_pairs = banks[b][:].rearrange("p (n i h) -> p n i h", n=HEADS_PER_BANK, h=2)
@@ -162,21 +183,8 @@ def tile_attention_pa_s_kernel(tc, x, w_qkv_words, w_qkv_scales, out_0, out_1, o
                     in1=sines[:, h, :].unsqueeze(1).to_broadcast([P, HEADS_PER_BANK, PAIRS]),
                     op=ALU.mult,
                 )
-            last = b == ROPE_BANKS - 1
-            adder = nc.vector if last else nc.gpsimd
-            pieces = 2 if last else 1
-            dest = q_flat[:, BANK * b : BANK * (b + 1)] if b < Q_HEADS // HEADS_PER_BANK else k_flat
-            rotated = work.tile([P, HEADS_PER_BANK, HEAD], F32)
-            heads = HEADS_PER_BANK // pieces
-            for piece in range(pieces):
-                n = slice(piece * heads, (piece + 1) * heads)
-                adder.tensor_tensor(
-                    out=rotated[:, n, :].rearrange("p n (i h) -> p (n i) h", h=2),
-                    in0=own[:, n, :].rearrange("p n (i h) -> p (n i) h", h=2),
-                    in1=other[:, :, n, :].rearrange("p h n i -> p (n i) h"),
-                    op=ALU.add,
-                )
-                nc.sync.dma_start(
-                    out=dest[:, HEAD * heads * piece : HEAD * heads * (piece + 1)],
-                    in_=rotated[:, n, :].rearrange("p n c -> p (n c)"),
-                )
+            products.append((own, other))
+            if b < GPSIMD_SUMS:
+                add_and_store(nc.gpsimd, b, 1)
+        for b in range(GPSIMD_SUMS, ROPE_BANKS):
+            add_and_store(nc.vector, b, 2 if b == ROPE_BANKS - 1 else 1)

@@ -122,8 +122,8 @@ def tile_attention_pa_s_kernel(tc, x, w_qkv_words, w_qkv_scales, out_0, out_1, o
             func=ACT.Sin,
             scale=TWO_PI,
         )
-        sines = keep.tile([P, 2, PAIRS], F32)
-        nc.scalar.activation(out=sines[:], in_=left[:, 1:3, :], func=ACT.Sin, scale=TWO_PI)
+        sines = keep.tile([P, PAIRS, 2], F32)
+        nc.scalar.activation(out=sines[:].rearrange("p i h -> p h i"), in_=left[:, 1:3, :], func=ACT.Sin, scale=TWO_PI)
 
         banks = []
         for b in range(N_ALL // BANK):
@@ -155,9 +155,9 @@ def tile_attention_pa_s_kernel(tc, x, w_qkv_words, w_qkv_scales, out_0, out_1, o
             for piece in range(pieces):
                 n = slice(piece * heads, (piece + 1) * heads)
                 adder.tensor_tensor(
-                    out=rotated[:, n, :].rearrange("p n (i h) -> p (n i) h", h=2),
-                    in0=own[:, n, :].rearrange("p n (i h) -> p (n i) h", h=2),
-                    in1=other[:, :, n, :].rearrange("p h n i -> p (n i) h"),
+                    out=rotated[:, n, :],
+                    in0=own[:, n, :],
+                    in1=other[:, n, :, :].rearrange("p n i h -> p n (i h)"),
                     op=ALU.add,
                 )
                 nc.sync.dma_start(
@@ -175,14 +175,13 @@ def tile_attention_pa_s_kernel(tc, x, w_qkv_words, w_qkv_scales, out_0, out_1, o
                 in1=cos_twice[:].rearrange("p i h -> p (i h)").unsqueeze(1).to_broadcast([P, HEADS_PER_BANK, HEAD]),
                 op=ALU.mult,
             )
-            other = work.tile([P, 2, HEADS_PER_BANK, PAIRS], F32)
-            for h in range(2):
-                nc.vector.tensor_tensor(
-                    out=other[:, h],
-                    in0=u_pairs[:, :, :, 1 - h],
-                    in1=sines[:, h, :].unsqueeze(1).to_broadcast([P, HEADS_PER_BANK, PAIRS]),
-                    op=ALU.mult,
-                )
+            other = work.tile([P, HEADS_PER_BANK, PAIRS, 2], F32)
+            nc.vector.tensor_tensor(
+                out=other[:],
+                in0=u_pairs[:, :, :, ::-1],
+                in1=sines[:].unsqueeze(1).to_broadcast([P, HEADS_PER_BANK, PAIRS, 2]),
+                op=ALU.mult,
+            )
             products.append((own, other))
             if b < GPSIMD_SUMS:
                 add_and_store(nc.gpsimd, b, 1)

@@ -26,6 +26,9 @@ THETA = 10000.0
 TWO_PI = 2.0 * math.pi
 WARM_MATMULS = 4
 GPSIMD_SUMS = 3
+KEEP_WARM_PASSES = 2
+TENSOR_SUM_HEADS = 2
+VECTOR_SUMS = ((3, 2, 4), (4, 0, 2), (4, 2, 4))
 
 FLOPS = 2 * P * DIM * N_ALL
 
@@ -126,10 +129,10 @@ def tile_attention_pa_s_kernel(tc, x, w_qkv_words, w_qkv_scales, out_0, out_1, o
         nc.scalar.activation(out=sines[:].rearrange("p i h -> p h i"), in_=left[:, 1:3, :], func=ACT.Sin, scale=TWO_PI)
 
         banks = []
-        for b in range(N_ALL // BANK):
-            acc = psum.tile([P, BANK], F32, name="acc%d" % b)
+
+        def multiply(b):
             nc.tensor.matmul_mx(
-                out=acc[:],
+                out=banks[b][:],
                 lhsT=x_codes[:].bitcast(FP8X4),
                 lhsT_scale=x_scales[:],
                 rhs=w_words[:, 2 * BANK * b : 2 * BANK * (b + 1)].bitcast(FP4X4),
@@ -137,7 +140,11 @@ def tile_attention_pa_s_kernel(tc, x, w_qkv_words, w_qkv_scales, out_0, out_1, o
                 start=True,
                 stop=True,
             )
+
+        for b in range(N_ALL // BANK):
+            acc = psum.tile([P, BANK], F32, name="acc%d" % b)
             banks.append(acc)
+            multiply(b)
 
         v_sb = keep.tile([P, BANK], F32)
         nc.scalar.copy(out=v_sb[:], in_=banks[ROPE_BANKS][:])
@@ -146,24 +153,21 @@ def tile_attention_pa_s_kernel(tc, x, w_qkv_words, w_qkv_scales, out_0, out_1, o
         q_flat = out_0.rearrange("t n d -> t (n d)")
         k_flat = out_1.rearrange("t n d -> t (n d)")
         products = []
+        results = []
 
-        def add_and_store(adder, b, pieces):
-            own, other = products[b]
+        def flat_heads(tile_of_heads, first, after):
+            return tile_of_heads[:, first:after].rearrange("p n c -> p (n c)")
+
+        def store(queue, b, first, after):
             dest = q_flat[:, BANK * b : BANK * (b + 1)] if b < Q_HEADS // HEADS_PER_BANK else k_flat
-            rotated = work.tile([P, HEADS_PER_BANK, HEAD], F32, name="rotated")
-            heads = HEADS_PER_BANK // pieces
-            for piece in range(pieces):
-                n = slice(piece * heads, (piece + 1) * heads)
-                adder.tensor_tensor(
-                    out=rotated[:, n, :],
-                    in0=own[:, n, :],
-                    in1=other[:, n, :, :].rearrange("p n i h -> p n (i h)"),
-                    op=ALU.add,
-                )
-                nc.sync.dma_start(
-                    out=dest[:, HEAD * heads * piece : HEAD * heads * (piece + 1)],
-                    in_=rotated[:, n, :].rearrange("p n c -> p (n c)"),
-                )
+            queue.dma_start(out=dest[:, HEAD * first : HEAD * after], in_=flat_heads(results[b], first, after))
+
+        def add_and_store(adder, queue, b, first, after):
+            own, other = products[b]
+            adder.tensor_tensor(
+                out=results[b][:, first:after], in0=own[:, first:after], in1=other[:, first:after], op=ALU.add
+            )
+            store(queue, b, first, after)
 
         for b in range(ROPE_BANKS):
             u_heads = banks[b][:].rearrange("p (n c) -> p n c", n=HEADS_PER_BANK)
@@ -175,15 +179,25 @@ def tile_attention_pa_s_kernel(tc, x, w_qkv_words, w_qkv_scales, out_0, out_1, o
                 in1=cos_twice[:].rearrange("p i h -> p (i h)").unsqueeze(1).to_broadcast([P, HEADS_PER_BANK, HEAD]),
                 op=ALU.mult,
             )
-            other = work.tile([P, HEADS_PER_BANK, PAIRS, 2], F32)
+            other = work.tile([P, HEADS_PER_BANK, HEAD], F32)
             nc.vector.tensor_tensor(
-                out=other[:],
+                out=other[:].rearrange("p n (i h) -> p n i h", h=2),
                 in0=u_pairs[:, :, :, ::-1],
                 in1=sines[:].unsqueeze(1).to_broadcast([P, HEADS_PER_BANK, PAIRS, 2]),
                 op=ALU.mult,
             )
             products.append((own, other))
+            rotated = work.tile([P, HEADS_PER_BANK, HEAD], F32)
+            results.append(rotated)
             if b < GPSIMD_SUMS:
-                add_and_store(nc.gpsimd, b, 1)
-        for b in range(GPSIMD_SUMS, ROPE_BANKS):
-            add_and_store(nc.vector, b, 2 if b == ROPE_BANKS - 1 else 1)
+                add_and_store(nc.gpsimd, nc.sync, b, 0, HEADS_PER_BANK)
+                for again in range(KEEP_WARM_PASSES):
+                    multiply(b)
+            if b == GPSIMD_SUMS:
+                summed = banks[0][:, 0 : HEAD * TENSOR_SUM_HEADS]
+                nc.tensor.matmul(summed, lhsT=ident[:], rhs=flat_heads(own, 0, TENSOR_SUM_HEADS), start=True, stop=False)
+                nc.tensor.matmul(summed, lhsT=ident[:], rhs=flat_heads(other, 0, TENSOR_SUM_HEADS), start=False, stop=True)
+                nc.scalar.copy(out=flat_heads(rotated, 0, TENSOR_SUM_HEADS), in_=summed)
+                store(nc.scalar, b, 0, TENSOR_SUM_HEADS)
+        for b, first, after in VECTOR_SUMS:
+            add_and_store(nc.vector, nc.sync, b, first, after)

@@ -48,6 +48,8 @@ def tile_attention_pa_s_kernel(tc, x, w_qkv_words, w_qkv_scales, out_0, out_1, o
             nc.sync.dma_start(out=w_words[:, cols].bitcast(I32), in_=w_qkv_words[0, :, cols].bitcast(I32))
 
         w_scales = keep.tile([P, N_ALL], U8, align_bytes=64)
+        freq = keep.tile([P, PAIRS], F32)
+        nc.vector.memset(freq[:, 0:1], 1.0)
         nc.vector.memset(w_scales[:].bitcast(I32), 0)
 
         load_words(0, 1)
@@ -69,31 +71,35 @@ def tile_attention_pa_s_kernel(tc, x, w_qkv_words, w_qkv_scales, out_0, out_1, o
         )
         ident = keep.tile([P, P], F32)
         make_identity(nc, ident[:])
-        shift = keep.tile([P, 3], F32)
-        nc.gpsimd.memset(shift[:], 0.0)
-        nc.gpsimd.memset(shift[:, 0:1], 0.25)
 
-        freq = keep.tile([P, 3, PAIRS], F32)
-        nc.vector.memset(freq[:, :, 0:1], 1.0)
-        nc.vector.memset(freq[:, 1, 0:1], -1.0)
         sin_first = keep.tile([P, 1], F32)
-        nc.scalar.activation(out=sin_first[:], in_=freq[:, 0, 0:1], func=ACT.Sin)
-        for level in (1, 4, 16):
-            for m in (1, 2, 3):
-                nc.vector.tensor_scalar(
-                    out=freq[:, :, m * level : (m + 1) * level],
-                    in0=freq[:, :, 0:level],
-                    scalar1=THETA ** (-m * level / PAIRS),
-                    scalar2=None,
-                    op0=ALU.mult,
-                )
+        nc.scalar.activation(out=sin_first[:], in_=freq[:, 0:1], func=ACT.Sin)
+
+        ratio = keep.tile([P, 1], F32)
+        nc.vector.tensor_scalar(
+            out=ratio[:], in0=freq[:, 0:1], scalar1=THETA ** (-1.0 / PAIRS), scalar2=None, op0=ALU.mult
+        )
+        zero = keep.tile([P, 1], F32)
+        nc.vector.memset(zero[:], 0.0)
+        shift = keep.tile([P, 3], F32)
+        nc.vector.memset(shift[:, 0:1], 0.25)
+        nc.vector.memset(shift[:, 1:2], 0.5)
+        nc.vector.memset(shift[:, 2:3], 0.0)
+        nc.vector.tensor_tensor_scan(
+            out=freq[:, 1:PAIRS],
+            data0=ratio[:].to_broadcast([P, PAIRS - 1]),
+            data1=zero[:].to_broadcast([P, PAIRS - 1]),
+            initial=1.0,
+            op0=ALU.mult,
+            op1=ALU.add,
+        )
         shift_wide = shift[:].unsqueeze(2).to_broadcast([P, 3, PAIRS])
         turns = keep.tile([P, 3, PAIRS], F32)
         whole = keep.tile([P, 3, PAIRS], I32)
         for rounded_or_not in (turns, whole):
             nc.vector.scalar_tensor_tensor(
                 out=rounded_or_not[:],
-                in0=freq[:],
+                in0=freq[:].unsqueeze(1).to_broadcast([P, 3, PAIRS]),
                 scalar=token_turns[:, 0:1],
                 in1=shift_wide,
                 op0=ALU.mult,

@@ -25,19 +25,15 @@ ROPE_BANKS = (Q_HEADS + KV_HEADS) // HEADS_PER_BANK
 THETA = 10000.0
 TWO_PI = 2.0 * math.pi
 WARM_MATMULS = 4
-GPSIMD_SUMS = 3
-KEEP_WARM_PASSES = 2
-TENSOR_SUM_HEADS = 2
-VECTOR_SUMS = ((3, 2, 4), (4, 0, 2), (4, 2, 4))
+V_BANK = ROPE_BANKS
+MULTIPLY_ORDER = (0, 1, 2, V_BANK, 3, 4)
 
 FLOPS = 2 * P * DIM * N_ALL
 
 
 def tile_attention_pa_s_kernel(tc, x, w_qkv_words, w_qkv_scales, out_0, out_1, out_2):
     nc = tc.nc
-    with tc.tile_pool(name="keep", bufs=1) as keep, tc.tile_pool(name="work", bufs=ROPE_BANKS) as work, tc.psum_pool(
-        name="psum", bufs=1
-    ) as psum, tc.manual_schedule():
+    with tc.tile_pool(name="keep", bufs=1) as keep, tc.psum_pool(name="psum", bufs=1) as psum, tc.manual_schedule():
         x_sb = keep.tile([P, DIM], BF16)
         nc.sync.dma_start(out=x_sb[:], in_=x)
 
@@ -48,8 +44,8 @@ def tile_attention_pa_s_kernel(tc, x, w_qkv_words, w_qkv_scales, out_0, out_1, o
             nc.sync.dma_start(out=w_words[:, cols].bitcast(I32), in_=w_qkv_words[0, :, cols].bitcast(I32))
 
         w_scales = keep.tile([P, N_ALL], U8, align_bytes=64)
-        freq = keep.tile([P, PAIRS], F32)
-        nc.vector.memset(freq[:, 0:1], 1.0)
+        steps = keep.tile([P, HEAD], F32)
+        nc.vector.memset(steps[:], -1.0)
         nc.vector.memset(w_scales[:].bitcast(I32), 0)
 
         load_words(0, 1)
@@ -63,54 +59,65 @@ def tile_attention_pa_s_kernel(tc, x, w_qkv_words, w_qkv_scales, out_0, out_1, o
 
         warm = keep.tile([P, P], F32)
         nc.gpsimd.memset(warm[:], 0.0)
-        token = keep.tile([P, 1], F32)
-        nc.gpsimd.iota(token[:], pattern=[[0, 1]], base=0, channel_multiplier=1, allow_small_or_imprecise_dtypes=True)
-        token_turns = keep.tile([P, 1], F32)
-        nc.gpsimd.tensor_scalar(
-            out=token_turns[:], in0=token[:], scalar1=1.0 / TWO_PI, scalar2=0.0, op0=ALU.mult, op1=ALU.add
-        )
         ident = keep.tile([P, P], F32)
         make_identity(nc, ident[:])
+        token = keep.tile([P, P], F32)
+        nc.gpsimd.iota(token[:], pattern=[[1, P]], base=0, channel_multiplier=0, allow_small_or_imprecise_dtypes=True)
+        swap = keep.tile([P, P], F32)
+        ident_pairs = ident[:].rearrange("p (i h) -> p i h", h=2)
+        swap_pairs = swap[:].rearrange("p (i h) -> p i h", h=2)
+        nc.gpsimd.tensor_copy(out=swap_pairs[:, :, 0], in_=ident_pairs[:, :, 1])
+        nc.gpsimd.tensor_copy(out=swap_pairs[:, :, 1], in_=ident_pairs[:, :, 0])
 
         sin_first = keep.tile([P, 1], F32)
-        nc.scalar.activation(out=sin_first[:], in_=freq[:, 0:1], func=ACT.Sin)
+        nc.scalar.activation(out=sin_first[:], in_=steps[:, 1:2], func=ACT.Sin)
 
-        ratio = keep.tile([P, 1], F32)
-        nc.vector.tensor_scalar(
-            out=ratio[:], in0=freq[:, 0:1], scalar1=THETA ** (-1.0 / PAIRS), scalar2=None, op0=ALU.mult
-        )
+        ratio = THETA ** (-1.0 / PAIRS)
+        nc.vector.tensor_scalar(out=steps[:, 0:HEAD:2], in0=steps[:, 1:HEAD:2], scalar1=ratio, scalar2=None, op0=ALU.mult)
         zero = keep.tile([P, 1], F32)
         nc.vector.memset(zero[:], 0.0)
-        shift = keep.tile([P, 3], F32)
+        shift = keep.tile([P, 2], F32)
         nc.vector.memset(shift[:, 0:1], 0.25)
-        nc.vector.memset(shift[:, 1:2], 0.5)
-        nc.vector.memset(shift[:, 2:3], 0.0)
+        nc.vector.memset(shift[:, 1:2], 0.0)
+        signed_row = keep.tile([P, HEAD], F32)
         nc.vector.tensor_tensor_scan(
-            out=freq[:, 1:PAIRS],
-            data0=ratio[:].to_broadcast([P, PAIRS - 1]),
-            data1=zero[:].to_broadcast([P, PAIRS - 1]),
-            initial=1.0,
+            out=signed_row[:],
+            data0=steps[:],
+            data1=zero[:].to_broadcast([P, HEAD]),
+            initial=-1.0 / (TWO_PI * ratio),
             op0=ALU.mult,
             op1=ALU.add,
         )
-        shift_wide = shift[:].unsqueeze(2).to_broadcast([P, 3, PAIRS])
-        turns = keep.tile([P, 3, PAIRS], F32)
-        whole = keep.tile([P, 3, PAIRS], I32)
+
+        picked = keep.tile([P, HEAD], F32)
+        signed_col = keep.tile([P, 1], F32)
+        nc.vector.scalar_tensor_tensor(
+            out=picked[:],
+            in0=ident[:],
+            scalar=1.0,
+            in1=signed_row[:],
+            op0=ALU.mult,
+            op1=ALU.mult,
+            accum_out=signed_col[:],
+        )
+        turns = keep.tile([P, 2, P], F32)
+        whole = keep.tile([P, 2, P], I32)
         for rounded_or_not in (turns, whole):
             nc.vector.scalar_tensor_tensor(
                 out=rounded_or_not[:],
-                in0=freq[:].unsqueeze(1).to_broadcast([P, 3, PAIRS]),
-                scalar=token_turns[:, 0:1],
-                in1=shift_wide,
+                in0=token[:].unsqueeze(1).to_broadcast([P, 2, P]),
+                scalar=signed_col[:, 0:1],
+                in1=shift[:].unsqueeze(2).to_broadcast([P, 2, P]),
                 op0=ALU.mult,
                 op1=ALU.add,
             )
-        left = keep.tile([P, 3, PAIRS], F32)
+        left = keep.tile([P, 2, P], F32)
         nc.vector.tensor_tensor(out=left[:], in0=turns[:], in1=whole[:], op=ALU.subtract)
 
         warm_out = psum.tile([P, P], F32)
         for i_warm in range(WARM_MATMULS):
             nc.tensor.matmul(warm_out[:], lhsT=warm[:], rhs=warm[:], start=True, stop=True)
+
         x_words = x_sb[:].bitcast(F32)
         x_t = psum.tile([P, 2, P], F32)
         for u in range(2):
@@ -124,86 +131,101 @@ def tile_attention_pa_s_kernel(tc, x, w_qkv_words, w_qkv_scales, out_0, out_1, o
         x_scales = keep.tile([P, P], U8, align_bytes=64)
         nc.vector.quantize_mx(out=x_codes[:].bitcast(FP8X4), scales=x_scales[:], in_=x_grouped[:])
 
-        cos_twice = keep.tile([P, PAIRS, 2], F32)
-        nc.scalar.activation(
-            out=cos_twice[:],
-            in_=left[:, 0, :].unsqueeze(2).to_broadcast([P, PAIRS, 2]),
-            func=ACT.Sin,
-            scale=TWO_PI,
-        )
-        sines = keep.tile([P, PAIRS, 2], F32)
-        nc.scalar.activation(out=sines[:].rearrange("p i h -> p h i"), in_=left[:, 1:3, :], func=ACT.Sin, scale=TWO_PI)
+        tables = keep.tile([P, 2, P], F32)
+        nc.scalar.activation(out=tables[:], in_=left[:], func=ACT.Sin, scale=TWO_PI)
 
         banks = []
-
-        def multiply(b):
-            nc.tensor.matmul_mx(
-                out=banks[b][:],
-                lhsT=x_codes[:].bitcast(FP8X4),
-                lhsT_scale=x_scales[:],
-                rhs=w_words[:, 2 * BANK * b : 2 * BANK * (b + 1)].bitcast(FP4X4),
-                rhs_scale=w_scales[:, BANK * b : BANK * (b + 1)],
-                start=True,
-                stop=True,
-            )
-
-        for b in range(N_ALL // BANK):
+        for b in range(ROPE_BANKS + 1):
             acc = psum.tile([P, BANK], F32, name="acc%d" % b)
             banks.append(acc)
-            multiply(b)
-
-        v_sb = keep.tile([P, BANK], F32)
-        nc.scalar.copy(out=v_sb[:], in_=banks[ROPE_BANKS][:])
-        nc.scalar.dma_start(out=out_2.rearrange("t n d -> t (n d)"), in_=v_sb[:])
+        for b in MULTIPLY_ORDER:
+            if b == V_BANK:
+                nc.tensor.matmul_mx(
+                    out=banks[b][:],
+                    lhsT=x_codes[:].bitcast(FP8X4),
+                    lhsT_scale=x_scales[:],
+                    rhs=w_words[:, 2 * BANK * b : 2 * BANK * (b + 1)].bitcast(FP4X4),
+                    rhs_scale=w_scales[:, BANK * b : BANK * (b + 1)],
+                    start=True,
+                    stop=True,
+                )
+            for n in range(HEADS_PER_BANK if b != V_BANK else 0):
+                head = HEADS_PER_BANK * b + n
+                nc.tensor.matmul_mx(
+                    out=banks[b][:, HEAD * n : HEAD * (n + 1)],
+                    lhsT=w_words[:, 2 * HEAD * head : 2 * HEAD * (head + 1)].bitcast(FP4X4),
+                    lhsT_scale=w_scales[:, HEAD * head : HEAD * (head + 1)],
+                    rhs=x_codes[:].bitcast(FP8X4),
+                    rhs_scale=x_scales[:],
+                    start=True,
+                    stop=True,
+                )
 
         q_flat = out_0.rearrange("t n d -> t (n d)")
         k_flat = out_1.rearrange("t n d -> t (n d)")
-        products = []
-        results = []
 
-        def flat_heads(tile_of_heads, first, after):
-            return tile_of_heads[:, first:after].rearrange("p n c -> p (n c)")
+        def heads_of(flat, first, after):
+            return flat[:, HEAD * first : HEAD * after].rearrange("p (n c) -> p n c", c=HEAD)
 
-        def store(queue, b, first, after):
-            dest = q_flat[:, BANK * b : BANK * (b + 1)] if b < Q_HEADS // HEADS_PER_BANK else k_flat
-            queue.dma_start(out=dest[:, HEAD * first : HEAD * after], in_=flat_heads(results[b], first, after))
+        def multiply_by_tables(engine, source, n_heads, label):
+            pair = []
+            for which in range(2):
+                product = keep.tile([P, n_heads, P], F32, name="product_%s_%d" % (label, which))
+                engine.tensor_tensor(
+                    out=product[:],
+                    in0=source,
+                    in1=tables[:, which, :].unsqueeze(1).to_broadcast([P, n_heads, P]),
+                    op=ALU.mult,
+                )
+                pair.append(product)
+            return pair
 
-        def add_and_store(adder, queue, b, first, after):
-            own, other = products[b]
-            adder.tensor_tensor(
-                out=results[b][:, first:after], in0=own[:, first:after], in1=other[:, first:after], op=ALU.add
-            )
-            store(queue, b, first, after)
+        def turn_and_add(pair, n_heads, target):
+            with_cos, with_sin = pair
+            for n in range(n_heads):
+                rotated = target[:, HEAD * n : HEAD * (n + 1)]
+                nc.tensor.matmul(rotated, lhsT=with_cos[:, n, :], rhs=ident[:], is_transpose=True, start=True, stop=False)
+                nc.tensor.matmul(rotated, lhsT=with_sin[:, n, :], rhs=swap[:], is_transpose=True, start=False, stop=True)
 
-        for b in range(ROPE_BANKS):
-            u_heads = banks[b][:].rearrange("p (n c) -> p n c", n=HEADS_PER_BANK)
-            u_pairs = banks[b][:].rearrange("p (n i h) -> p n i h", n=HEADS_PER_BANK, h=2)
-            own = work.tile([P, HEADS_PER_BANK, HEAD], F32)
-            nc.vector.tensor_tensor(
-                out=own[:],
-                in0=u_heads,
-                in1=cos_twice[:].rearrange("p i h -> p (i h)").unsqueeze(1).to_broadcast([P, HEADS_PER_BANK, HEAD]),
-                op=ALU.mult,
-            )
-            other = work.tile([P, HEADS_PER_BANK, HEAD], F32)
-            nc.vector.tensor_tensor(
-                out=other[:].rearrange("p n (i h) -> p n i h", h=2),
-                in0=u_pairs[:, :, :, ::-1],
-                in1=sines[:].unsqueeze(1).to_broadcast([P, HEADS_PER_BANK, PAIRS, 2]),
-                op=ALU.mult,
-            )
-            products.append((own, other))
-            rotated = work.tile([P, HEADS_PER_BANK, HEAD], F32)
-            results.append(rotated)
-            if b < GPSIMD_SUMS:
-                add_and_store(nc.gpsimd, nc.sync, b, 0, HEADS_PER_BANK)
-                for again in range(KEEP_WARM_PASSES):
-                    multiply(b)
-            if b == GPSIMD_SUMS:
-                summed = banks[0][:, 0 : HEAD * TENSOR_SUM_HEADS]
-                nc.tensor.matmul(summed, lhsT=ident[:], rhs=flat_heads(own, 0, TENSOR_SUM_HEADS), start=True, stop=False)
-                nc.tensor.matmul(summed, lhsT=ident[:], rhs=flat_heads(other, 0, TENSOR_SUM_HEADS), start=False, stop=True)
-                nc.scalar.copy(out=flat_heads(rotated, 0, TENSOR_SUM_HEADS), in_=summed)
-                store(nc.scalar, b, 0, TENSOR_SUM_HEADS)
-        for b, first, after in VECTOR_SUMS:
-            add_and_store(nc.vector, nc.sync, b, first, after)
+        def leave(copy, target, n_heads, first_head, label):
+            result = keep.tile([P, HEAD * n_heads], F32, name="result_%s" % label)
+            copy(out=result[:], in_=target[:, 0 : HEAD * n_heads])
+            if first_head < Q_HEADS:
+                dest = q_flat[:, HEAD * first_head : HEAD * (first_head + n_heads)]
+            else:
+                dest = k_flat[:, HEAD * (first_head - Q_HEADS) : HEAD * (first_head - Q_HEADS + n_heads)]
+            nc.sync.dma_start(out=dest, in_=result[:])
+
+        for_gpsimd = keep.tile([P, BANK + HEAD], F32)
+        nc.scalar.copy(out=for_gpsimd[:, 0:BANK], in_=banks[1][:])
+        pair_v0 = multiply_by_tables(nc.vector, heads_of(banks[0][:], 0, 4), 4, "v0")
+        pair_g1a = multiply_by_tables(nc.gpsimd, heads_of(for_gpsimd[:], 0, 2), 2, "g1a")
+        turn_and_add(pair_v0, 4, banks[0][:])
+        v_sb = keep.tile([P, BANK], F32)
+        nc.scalar.copy(out=v_sb[:], in_=banks[V_BANK][:])
+        nc.scalar.dma_start(out=out_2.rearrange("t n d -> t (n d)"), in_=v_sb[:])
+        leave(nc.scalar.copy, banks[0][:], 4, 0, "v0")
+        nc.scalar.copy(out=for_gpsimd[:, BANK : BANK + HEAD], in_=banks[4][:, 3 * HEAD : 4 * HEAD])
+
+        pair_v2 = multiply_by_tables(nc.vector, heads_of(banks[2][:], 0, 4), 4, "v2")
+        turn_and_add(pair_v2, 4, banks[2][:])
+        leave(nc.scalar.copy, banks[2][:], 4, 8, "v2")
+        turn_and_add(pair_g1a, 2, banks[1][:, 0 : 2 * HEAD])
+        leave(nc.scalar.copy, banks[1][:, 0 : 2 * HEAD], 2, 4, "g1a")
+
+        pair_v3 = multiply_by_tables(nc.vector, heads_of(banks[3][:], 0, 4), 4, "v3")
+        pair_g1b = multiply_by_tables(nc.gpsimd, heads_of(for_gpsimd[:], 2, 4), 2, "g1b")
+        turn_and_add(pair_v3, 4, banks[3][:])
+        leave(nc.scalar.copy, banks[3][:], 4, 12, "v3")
+        turn_and_add(pair_g1b, 2, banks[1][:, 2 * HEAD : 4 * HEAD])
+        leave(nc.scalar.copy, banks[1][:, 2 * HEAD : 4 * HEAD], 2, 6, "g1b")
+
+        pair_v4a = multiply_by_tables(nc.vector, heads_of(banks[4][:], 0, 2), 2, "v4a")
+        pair_v4b = multiply_by_tables(nc.vector, heads_of(banks[4][:], 2, 3), 1, "v4b")
+        pair_g4c = multiply_by_tables(nc.gpsimd, heads_of(for_gpsimd[:], 4, 5), 1, "g4c")
+        turn_and_add(pair_v4a, 2, x_t[:].rearrange("p u t -> p (u t)"))
+        leave(nc.vector.tensor_copy, x_t[:].rearrange("p u t -> p (u t)"), 2, 16, "v4a")
+        turn_and_add(pair_v4b, 1, warm_out[:])
+        leave(nc.vector.tensor_copy, warm_out[:], 1, 18, "v4b")
+        turn_and_add(pair_g4c, 1, banks[V_BANK][:, 0:HEAD])
+        leave(nc.scalar.copy, banks[V_BANK][:, 0:HEAD], 1, 19, "g4c")

@@ -187,6 +187,9 @@ def tile_attention_pa_s_kernel(tc, x, w_qkv_words, w_qkv_scales, out_0, out_1, o
                 nc.tensor.matmul(rotated, lhsT=with_cos[:, n, :], rhs=ident[:], is_transpose=True, start=True, stop=False)
                 nc.tensor.matmul(rotated, lhsT=with_sin[:, n, :], rhs=swap[:], is_transpose=True, start=False, stop=True)
 
+        def keep_clock_up():
+            nc.tensor.matmul(warm_out[:], lhsT=warm[:], rhs=warm[:], start=True, stop=True)
+
         def leave(copy, target, n_heads, first_head, label):
             result = keep.tile([P, HEAD * n_heads], F32, name="result_%s" % label)
             copy(out=result[:], in_=target[:, 0 : HEAD * n_heads])
@@ -201,6 +204,7 @@ def tile_attention_pa_s_kernel(tc, x, w_qkv_words, w_qkv_scales, out_0, out_1, o
         pair_v0 = multiply_by_tables(nc.vector, heads_of(banks[0][:], 0, 4), 4, "v0")
         pair_g1a = multiply_by_tables(nc.gpsimd, heads_of(for_gpsimd[:], 0, 2), 2, "g1a")
         turn_and_add(pair_v0, 4, banks[0][:])
+        keep_clock_up()
         v_sb = keep.tile([P, BANK], F32)
         nc.scalar.copy(out=v_sb[:], in_=banks[V_BANK][:])
         nc.scalar.dma_start(out=out_2.rearrange("t n d -> t (n d)"), in_=v_sb[:])
@@ -209,15 +213,19 @@ def tile_attention_pa_s_kernel(tc, x, w_qkv_words, w_qkv_scales, out_0, out_1, o
 
         pair_v2 = multiply_by_tables(nc.vector, heads_of(banks[2][:], 0, 4), 4, "v2")
         turn_and_add(pair_v2, 4, banks[2][:])
+        keep_clock_up()
         leave(nc.scalar.copy, banks[2][:], 4, 8, "v2")
         turn_and_add(pair_g1a, 2, banks[1][:, 0 : 2 * HEAD])
+        keep_clock_up()
         leave(nc.scalar.copy, banks[1][:, 0 : 2 * HEAD], 2, 4, "g1a")
 
         pair_v3 = multiply_by_tables(nc.vector, heads_of(banks[3][:], 0, 4), 4, "v3")
         pair_g1b = multiply_by_tables(nc.gpsimd, heads_of(for_gpsimd[:], 2, 4), 2, "g1b")
         turn_and_add(pair_v3, 4, banks[3][:])
+        keep_clock_up()
         leave(nc.scalar.copy, banks[3][:], 4, 12, "v3")
         turn_and_add(pair_g1b, 2, banks[1][:, 2 * HEAD : 4 * HEAD])
+        keep_clock_up()
         leave(nc.scalar.copy, banks[1][:, 2 * HEAD : 4 * HEAD], 2, 6, "g1b")
 
         pair_v4a = multiply_by_tables(nc.vector, heads_of(banks[4][:], 0, 2), 2, "v4a")

@@ -26,7 +26,7 @@ THETA = 10000.0
 TWO_PI = 2.0 * math.pi
 WARM_MATMULS = 4
 V_BANK = ROPE_BANKS
-MULTIPLY_ORDER = (0, 1, 2, V_BANK, 3, 4)
+K_BANK = ROPE_BANKS - 1
 
 FLOPS = 2 * P * DIM * N_ALL
 
@@ -45,7 +45,6 @@ def tile_attention_pa_s_kernel(tc, x, w_qkv_words, w_qkv_scales, out_0, out_1, o
 
         w_scales = keep.tile([P, N_ALL], U8, align_bytes=64)
         steps = keep.tile([P, HEAD], F32)
-        nc.vector.memset(steps[:], -1.0)
         nc.vector.memset(w_scales[:].bitcast(I32), 0)
 
         load_words(0, 1)
@@ -59,6 +58,11 @@ def tile_attention_pa_s_kernel(tc, x, w_qkv_words, w_qkv_scales, out_0, out_1, o
 
         warm = keep.tile([P, P], F32)
         nc.gpsimd.memset(warm[:], 0.0)
+        ratio = THETA ** (-1.0 / PAIRS)
+        nc.gpsimd.memset(steps[:], -1.0)
+        nc.gpsimd.tensor_scalar(
+            out=steps[:, 0:HEAD:2], in0=steps[:, 1:HEAD:2], scalar1=ratio, scalar2=0.0, op0=ALU.mult, op1=ALU.add
+        )
         ident = keep.tile([P, P], F32)
         make_identity(nc, ident[:])
         token = keep.tile([P, P], F32)
@@ -70,24 +74,20 @@ def tile_attention_pa_s_kernel(tc, x, w_qkv_words, w_qkv_scales, out_0, out_1, o
         nc.gpsimd.tensor_copy(out=swap_pairs[:, :, 1], in_=ident_pairs[:, :, 0])
 
         sin_first = keep.tile([P, 1], F32)
-        nc.scalar.activation(out=sin_first[:], in_=steps[:, 1:2], func=ACT.Sin)
+        nc.scalar.activation(out=sin_first[:], in_=warm[:, 0:1], func=ACT.Sin)
 
-        ratio = THETA ** (-1.0 / PAIRS)
-        nc.vector.tensor_scalar(out=steps[:, 0:HEAD:2], in0=steps[:, 1:HEAD:2], scalar1=ratio, scalar2=None, op0=ALU.mult)
-        zero = keep.tile([P, 1], F32)
-        nc.vector.memset(zero[:], 0.0)
-        shift = keep.tile([P, 2], F32)
-        nc.vector.memset(shift[:, 0:1], 0.25)
-        nc.vector.memset(shift[:, 1:2], 0.0)
         signed_row = keep.tile([P, HEAD], F32)
         nc.vector.tensor_tensor_scan(
             out=signed_row[:],
             data0=steps[:],
-            data1=zero[:].to_broadcast([P, HEAD]),
+            data1=warm[:, 0:1].to_broadcast([P, HEAD]),
             initial=-1.0 / (TWO_PI * ratio),
             op0=ALU.mult,
             op1=ALU.add,
         )
+        shift = keep.tile([P, 2], F32)
+        nc.vector.memset(shift[:, 0:1], 0.25)
+        nc.vector.memset(shift[:, 1:2], 0.0)
 
         picked = keep.tile([P, HEAD], F32)
         signed_col = keep.tile([P, 1], F32)
@@ -138,18 +138,9 @@ def tile_attention_pa_s_kernel(tc, x, w_qkv_words, w_qkv_scales, out_0, out_1, o
         for b in range(ROPE_BANKS + 1):
             acc = psum.tile([P, BANK], F32, name="acc%d" % b)
             banks.append(acc)
-        for b in MULTIPLY_ORDER:
-            if b == V_BANK:
-                nc.tensor.matmul_mx(
-                    out=banks[b][:],
-                    lhsT=x_codes[:].bitcast(FP8X4),
-                    lhsT_scale=x_scales[:],
-                    rhs=w_words[:, 2 * BANK * b : 2 * BANK * (b + 1)].bitcast(FP4X4),
-                    rhs_scale=w_scales[:, BANK * b : BANK * (b + 1)],
-                    start=True,
-                    stop=True,
-                )
-            for n in range(HEADS_PER_BANK if b != V_BANK else 0):
+
+        def features_on_partitions(b, first, after):
+            for n in range(first, after):
                 head = HEADS_PER_BANK * b + n
                 nc.tensor.matmul_mx(
                     out=banks[b][:, HEAD * n : HEAD * (n + 1)],
@@ -160,6 +151,17 @@ def tile_attention_pa_s_kernel(tc, x, w_qkv_words, w_qkv_scales, out_0, out_1, o
                     start=True,
                     stop=True,
                 )
+
+        def tokens_on_partitions(b):
+            nc.tensor.matmul_mx(
+                out=banks[b][:],
+                lhsT=x_codes[:].bitcast(FP8X4),
+                lhsT_scale=x_scales[:],
+                rhs=w_words[:, 2 * BANK * b : 2 * BANK * (b + 1)].bitcast(FP4X4),
+                rhs_scale=w_scales[:, BANK * b : BANK * (b + 1)],
+                start=True,
+                stop=True,
+            )
 
         q_flat = out_0.rearrange("t n d -> t (n d)")
         k_flat = out_1.rearrange("t n d -> t (n d)")
@@ -190,50 +192,87 @@ def tile_attention_pa_s_kernel(tc, x, w_qkv_words, w_qkv_scales, out_0, out_1, o
         def keep_clock_up():
             nc.tensor.matmul(warm_out[:], lhsT=warm[:], rhs=warm[:], start=True, stop=True)
 
-        def leave(copy, target, n_heads, first_head, label):
+        def leave(target, n_heads, first_head, label):
             result = keep.tile([P, HEAD * n_heads], F32, name="result_%s" % label)
-            copy(out=result[:], in_=target[:, 0 : HEAD * n_heads])
-            if first_head < Q_HEADS:
-                dest = q_flat[:, HEAD * first_head : HEAD * (first_head + n_heads)]
-            else:
-                dest = k_flat[:, HEAD * (first_head - Q_HEADS) : HEAD * (first_head - Q_HEADS + n_heads)]
-            nc.sync.dma_start(out=dest, in_=result[:])
+            nc.scalar.copy(out=result[:], in_=target[:, 0 : HEAD * n_heads])
+            nc.sync.dma_start(out=q_flat[:, HEAD * first_head : HEAD * (first_head + n_heads)], in_=result[:])
 
-        for_gpsimd = keep.tile([P, BANK + HEAD], F32)
-        nc.scalar.copy(out=for_gpsimd[:, 0:BANK], in_=banks[1][:])
-        pair_v0 = multiply_by_tables(nc.vector, heads_of(banks[0][:], 0, 4), 4, "v0")
-        pair_g1a = multiply_by_tables(nc.gpsimd, heads_of(for_gpsimd[:], 0, 2), 2, "g1a")
-        turn_and_add(pair_v0, 4, banks[0][:])
-        keep_clock_up()
+        features_on_partitions(0, 0, 4)
+        features_on_partitions(1, 0, 4)
+        features_on_partitions(2, 0, 4)
+        tables_turned = x_t
+        nc.tensor.transpose(tables_turned[:, 0, :], tables[:, 0, :], ident[:])
+        nc.tensor.transpose(tables_turned[:, 1, :], tables[:, 1, :], swap[:])
+        tokens_on_partitions(V_BANK)
+        features_on_partitions(3, 0, 4)
+
+        for_gpsimd = keep.tile([P, BANK], F32)
+        nc.scalar.copy(out=for_gpsimd[:], in_=banks[1][:])
         v_sb = keep.tile([P, BANK], F32)
         nc.scalar.copy(out=v_sb[:], in_=banks[V_BANK][:])
-        nc.scalar.dma_start(out=out_2.rearrange("t n d -> t (n d)"), in_=v_sb[:])
-        leave(nc.scalar.copy, banks[0][:], 4, 0, "v0")
-        nc.scalar.copy(out=for_gpsimd[:, BANK : BANK + HEAD], in_=banks[4][:, 3 * HEAD : 4 * HEAD])
+        nc.sync.dma_start(out=out_2.rearrange("t n d -> t (n d)"), in_=v_sb[:])
+        by_token = keep.tile([P, 2, P], F32)
+        nc.scalar.copy(out=by_token[:], in_=tables_turned[:])
 
-        pair_v2 = multiply_by_tables(nc.vector, heads_of(banks[2][:], 0, 4), 4, "v2")
-        turn_and_add(pair_v2, 4, banks[2][:])
-        keep_clock_up()
-        leave(nc.scalar.copy, banks[2][:], 4, 8, "v2")
-        turn_and_add(pair_g1a, 2, banks[1][:, 0 : 2 * HEAD])
-        keep_clock_up()
-        leave(nc.scalar.copy, banks[1][:, 0 : 2 * HEAD], 2, 4, "g1a")
+        pairs = {}
+        for b, half in ((0, 0), (0, 1), (1, 0), (2, 0), (2, 1), (1, 1), (3, 0), (3, 1)):
+            if b == 1:
+                pairs[(b, half)] = multiply_by_tables(nc.gpsimd, heads_of(for_gpsimd[:], 2 * half, 2 * half + 2), 2, "g%d" % half)
+            else:
+                pairs[(b, half)] = multiply_by_tables(
+                    nc.vector, heads_of(banks[b][:], 2 * half, 2 * half + 2), 2, "u%d_%d" % (b, half)
+                )
 
-        pair_v3 = multiply_by_tables(nc.vector, heads_of(banks[3][:], 0, 4), 4, "v3")
-        pair_g1b = multiply_by_tables(nc.gpsimd, heads_of(for_gpsimd[:], 2, 4), 2, "g1b")
-        turn_and_add(pair_v3, 4, banks[3][:])
-        keep_clock_up()
-        leave(nc.scalar.copy, banks[3][:], 4, 12, "v3")
-        turn_and_add(pair_g1b, 2, banks[1][:, 2 * HEAD : 4 * HEAD])
-        keep_clock_up()
-        leave(nc.scalar.copy, banks[1][:, 2 * HEAD : 4 * HEAD], 2, 6, "g1b")
+        u_heads = banks[K_BANK][:].rearrange("p (n c) -> p n c", n=HEADS_PER_BANK)
+        u_pairs = banks[K_BANK][:].rearrange("p (n i h) -> p n i h", n=HEADS_PER_BANK, h=2)
+        own = keep.tile([P, HEADS_PER_BANK, HEAD], F32)
+        other = keep.tile([P, HEADS_PER_BANK, HEAD], F32)
+        rotated_k = keep.tile([P, HEADS_PER_BANK, HEAD], F32)
 
-        pair_v4a = multiply_by_tables(nc.vector, heads_of(banks[4][:], 0, 2), 2, "v4a")
-        pair_v4b = multiply_by_tables(nc.vector, heads_of(banks[4][:], 2, 3), 1, "v4b")
-        pair_g4c = multiply_by_tables(nc.gpsimd, heads_of(for_gpsimd[:], 4, 5), 1, "g4c")
-        turn_and_add(pair_v4a, 2, x_t[:].rearrange("p u t -> p (u t)"))
-        leave(nc.vector.tensor_copy, x_t[:].rearrange("p u t -> p (u t)"), 2, 16, "v4a")
-        turn_and_add(pair_v4b, 1, warm_out[:])
-        leave(nc.vector.tensor_copy, warm_out[:], 1, 18, "v4b")
-        turn_and_add(pair_g4c, 1, banks[V_BANK][:, 0:HEAD])
-        leave(nc.scalar.copy, banks[V_BANK][:, 0:HEAD], 1, 19, "g4c")
+        def multiply_k(first, after):
+            n_heads = after - first
+            nc.vector.tensor_tensor(
+                out=own[:, first:after],
+                in0=u_heads[:, first:after],
+                in1=by_token[:, 0, :].unsqueeze(1).to_broadcast([P, n_heads, HEAD]),
+                op=ALU.mult,
+            )
+            nc.vector.tensor_tensor(
+                out=other[:, first:after].rearrange("p n (i h) -> p n i h", h=2),
+                in0=u_pairs[:, first:after, :, ::-1],
+                in1=by_token[:, 1, :].rearrange("p (i h) -> p i h", h=2).unsqueeze(1).to_broadcast([P, n_heads, PAIRS, 2]),
+                op=ALU.mult,
+            )
+
+        def add_and_store_k(first, after):
+            nc.vector.tensor_tensor(
+                out=rotated_k[:, first:after], in0=own[:, first:after], in1=other[:, first:after], op=ALU.add
+            )
+            nc.sync.dma_start(
+                out=k_flat[:, HEAD * first : HEAD * after], in_=rotated_k[:, first:after].rearrange("p n c -> p (n c)")
+            )
+
+        targets = (1, 0, V_BANK)
+
+        def finish(i_piece, b, half):
+            target = banks[targets[i_piece % 3]][:, 0 : 2 * HEAD]
+            turn_and_add(pairs[(b, half)], 2, target)
+            leave(target, 2, HEADS_PER_BANK * b + 2 * half, "%d_%d" % (b, half))
+
+        finish(0, 0, 0)
+        finish(1, 0, 1)
+        tokens_on_partitions(K_BANK)
+        finish(2, 2, 0)
+        keep_clock_up()
+        finish(3, 2, 1)
+        keep_clock_up()
+        finish(4, 1, 0)
+        finish(5, 3, 0)
+        keep_clock_up()
+        multiply_k(0, 2)
+        multiply_k(2, 4)
+        add_and_store_k(0, 2)
+        finish(6, 3, 1)
+        keep_clock_up()
+        add_and_store_k(2, 4)
+        finish(7, 1, 1)

@@ -54,7 +54,8 @@ def tile_attention_pa_s_kernel(tc, x, w_qkv_words, w_qkv_scales, out_0, out_1, o
                 in_=w_qkv_scales[0, 4 * quadrant : 4 * quadrant + 4, :].bitcast(I32),
             )
         load_words(1, 2)
-        load_words(3, 3)
+        load_words(3, 1)
+        load_words(4, 2)
 
         warm = keep.tile([P, P], F32)
         nc.gpsimd.memset(warm[:], 0.0)
@@ -152,13 +153,15 @@ def tile_attention_pa_s_kernel(tc, x, w_qkv_words, w_qkv_scales, out_0, out_1, o
                     stop=True,
                 )
 
-        def tokens_on_partitions(b):
+        def tokens_on_partitions(b, first, after):
+            head = HEADS_PER_BANK * b + first
+            n_heads = after - first
             nc.tensor.matmul_mx(
-                out=banks[b][:],
+                out=banks[b][:, HEAD * first : HEAD * after],
                 lhsT=x_codes[:].bitcast(FP8X4),
                 lhsT_scale=x_scales[:],
-                rhs=w_words[:, 2 * BANK * b : 2 * BANK * (b + 1)].bitcast(FP4X4),
-                rhs_scale=w_scales[:, BANK * b : BANK * (b + 1)],
+                rhs=w_words[:, 2 * HEAD * head : 2 * HEAD * (head + n_heads)].bitcast(FP4X4),
+                rhs_scale=w_scales[:, HEAD * head : HEAD * (head + n_heads)],
                 start=True,
                 stop=True,
             )
@@ -203,19 +206,21 @@ def tile_attention_pa_s_kernel(tc, x, w_qkv_words, w_qkv_scales, out_0, out_1, o
         tables_turned = x_t
         nc.tensor.transpose(tables_turned[:, 0, :], tables[:, 0, :], ident[:])
         nc.tensor.transpose(tables_turned[:, 1, :], tables[:, 1, :], swap[:])
-        tokens_on_partitions(V_BANK)
-        features_on_partitions(3, 0, 4)
+        tokens_on_partitions(3, 0, 4)
+        tokens_on_partitions(V_BANK, 0, 4)
+        tokens_on_partitions(K_BANK, 0, 4)
 
         for_gpsimd = keep.tile([P, BANK], F32)
-        nc.scalar.copy(out=for_gpsimd[:], in_=banks[1][:])
+        nc.scalar.copy(out=for_gpsimd[:, 0 : 2 * HEAD], in_=banks[1][:, 0 : 2 * HEAD])
+        nc.scalar.copy(out=for_gpsimd[:, 2 * HEAD : BANK], in_=banks[1][:, 2 * HEAD : BANK])
+        by_token = keep.tile([P, 2, P], F32)
+        nc.scalar.copy(out=by_token[:], in_=tables_turned[:])
         v_sb = keep.tile([P, BANK], F32)
         nc.scalar.copy(out=v_sb[:], in_=banks[V_BANK][:])
         nc.sync.dma_start(out=out_2.rearrange("t n d -> t (n d)"), in_=v_sb[:])
-        by_token = keep.tile([P, 2, P], F32)
-        nc.scalar.copy(out=by_token[:], in_=tables_turned[:])
 
         pairs = {}
-        for b, half in ((0, 0), (0, 1), (1, 0), (2, 0), (2, 1), (1, 1), (3, 0), (3, 1)):
+        for b, half in ((0, 0), (0, 1), (1, 0), (2, 0), (2, 1), (1, 1)):
             if b == 1:
                 pairs[(b, half)] = multiply_by_tables(nc.gpsimd, heads_of(for_gpsimd[:], 2 * half, 2 * half + 2), 2, "g%d" % half)
             else:
@@ -223,34 +228,30 @@ def tile_attention_pa_s_kernel(tc, x, w_qkv_words, w_qkv_scales, out_0, out_1, o
                     nc.vector, heads_of(banks[b][:], 2 * half, 2 * half + 2), 2, "u%d_%d" % (b, half)
                 )
 
-        u_heads = banks[K_BANK][:].rearrange("p (n c) -> p n c", n=HEADS_PER_BANK)
-        u_pairs = banks[K_BANK][:].rearrange("p (n i h) -> p n i h", n=HEADS_PER_BANK, h=2)
-        own = keep.tile([P, HEADS_PER_BANK, HEAD], F32)
-        other = keep.tile([P, HEADS_PER_BANK, HEAD], F32)
-        rotated_k = keep.tile([P, HEADS_PER_BANK, HEAD], F32)
+        LATE = 4
+        own = keep.tile([P, 2 * LATE, HEAD], F32)
+        other = keep.tile([P, 2 * LATE, HEAD], F32)
+        rotated_late = keep.tile([P, 2 * LATE, HEAD], F32)
 
-        def multiply_k(first, after):
-            n_heads = after - first
+        def multiply_late(i_late, source):
+            heads = slice(2 * i_late, 2 * i_late + 2)
             nc.vector.tensor_tensor(
-                out=own[:, first:after],
-                in0=u_heads[:, first:after],
-                in1=by_token[:, 0, :].unsqueeze(1).to_broadcast([P, n_heads, HEAD]),
+                out=own[:, heads],
+                in0=source.rearrange("p (n c) -> p n c", n=2),
+                in1=by_token[:, 0, :].unsqueeze(1).to_broadcast([P, 2, HEAD]),
                 op=ALU.mult,
             )
             nc.vector.tensor_tensor(
-                out=other[:, first:after].rearrange("p n (i h) -> p n i h", h=2),
-                in0=u_pairs[:, first:after, :, ::-1],
-                in1=by_token[:, 1, :].rearrange("p (i h) -> p i h", h=2).unsqueeze(1).to_broadcast([P, n_heads, PAIRS, 2]),
+                out=other[:, heads].rearrange("p n (i h) -> p n i h", h=2),
+                in0=source.rearrange("p (n i h) -> p n i h", n=2, h=2)[:, :, :, ::-1],
+                in1=by_token[:, 1, :].rearrange("p (i h) -> p i h", h=2).unsqueeze(1).to_broadcast([P, 2, PAIRS, 2]),
                 op=ALU.mult,
             )
 
-        def add_and_store_k(first, after):
-            nc.vector.tensor_tensor(
-                out=rotated_k[:, first:after], in0=own[:, first:after], in1=other[:, first:after], op=ALU.add
-            )
-            nc.sync.dma_start(
-                out=k_flat[:, HEAD * first : HEAD * after], in_=rotated_k[:, first:after].rearrange("p n c -> p (n c)")
-            )
+        def add_and_store_late(i_late, dest):
+            heads = slice(2 * i_late, 2 * i_late + 2)
+            nc.vector.tensor_tensor(out=rotated_late[:, heads], in0=own[:, heads], in1=other[:, heads], op=ALU.add)
+            nc.sync.dma_start(out=dest, in_=rotated_late[:, heads].rearrange("p n c -> p (n c)"))
 
         targets = (1, 0, V_BANK)
 
@@ -261,18 +262,19 @@ def tile_attention_pa_s_kernel(tc, x, w_qkv_words, w_qkv_scales, out_0, out_1, o
 
         finish(0, 0, 0)
         finish(1, 0, 1)
-        tokens_on_partitions(K_BANK)
-        finish(2, 2, 0)
         keep_clock_up()
+        finish(2, 2, 0)
         finish(3, 2, 1)
         keep_clock_up()
+        multiply_late(0, banks[3][:, 0 : 2 * HEAD])
+        multiply_late(1, banks[3][:, 2 * HEAD : BANK])
+        add_and_store_late(0, q_flat[:, HEAD * 12 : HEAD * 14])
         finish(4, 1, 0)
-        finish(5, 3, 0)
         keep_clock_up()
-        multiply_k(0, 2)
-        multiply_k(2, 4)
-        add_and_store_k(0, 2)
-        finish(6, 3, 1)
         keep_clock_up()
-        add_and_store_k(2, 4)
-        finish(7, 1, 1)
+        multiply_late(2, banks[K_BANK][:, 0 : 2 * HEAD])
+        add_and_store_late(1, q_flat[:, HEAD * 14 : HEAD * 16])
+        multiply_late(3, banks[K_BANK][:, 2 * HEAD : BANK])
+        add_and_store_late(2, k_flat[:, 0 : 2 * HEAD])
+        add_and_store_late(3, k_flat[:, 2 * HEAD : BANK])
+        finish(5, 1, 1)

@@ -24,7 +24,8 @@ HEADS_PER_BANK = BANK // HEAD
 ROPE_BANKS = (Q_HEADS + KV_HEADS) // HEADS_PER_BANK
 THETA = 10000.0
 TWO_PI = 2.0 * math.pi
-WARM_MATMULS = 4
+WARM_MATMULS = 3
+BRIDGE_MATMULS = 2
 V_BANK = ROPE_BANKS
 K_BANK = ROPE_BANKS - 1
 
@@ -123,6 +124,8 @@ def tile_attention_pa_s_kernel(tc, x, w_qkv_words, w_qkv_scales, out_0, out_1, o
         x_t = psum.tile([P, 2, P], F32)
         for u in range(2):
             nc.tensor.transpose(x_t[:, u, :], x_words[:, u : DIM // 2 : 2], ident[:])
+        for i_warm in range(BRIDGE_MATMULS):
+            nc.tensor.matmul(warm_out[:], lhsT=warm[:], rhs=warm[:], start=True, stop=True)
         x_grouped = keep.tile([P, 4 * P], BF16, align_bytes=64)
         nc.scalar.copy(
             out=x_grouped[:].bitcast(F32).rearrange("p (t u) -> p t u", u=2),
@@ -266,15 +269,15 @@ def tile_attention_pa_s_kernel(tc, x, w_qkv_words, w_qkv_scales, out_0, out_1, o
         finish(2, 2, 0)
         finish(3, 2, 1)
         keep_clock_up()
-        multiply_late(0, banks[3][:, 0 : 2 * HEAD])
-        multiply_late(1, banks[3][:, 2 * HEAD : BANK])
-        add_and_store_late(0, q_flat[:, HEAD * 12 : HEAD * 14])
         finish(4, 1, 0)
         keep_clock_up()
         keep_clock_up()
+        multiply_late(0, banks[3][:, 0 : 2 * HEAD])
+        multiply_late(1, banks[3][:, 2 * HEAD : BANK])
         multiply_late(2, banks[K_BANK][:, 0 : 2 * HEAD])
-        add_and_store_late(1, q_flat[:, HEAD * 14 : HEAD * 16])
         multiply_late(3, banks[K_BANK][:, 2 * HEAD : BANK])
+        add_and_store_late(0, q_flat[:, HEAD * 12 : HEAD * 14])
+        add_and_store_late(1, q_flat[:, HEAD * 14 : HEAD * 16])
         add_and_store_late(2, k_flat[:, 0 : 2 * HEAD])
-        add_and_store_late(3, k_flat[:, 2 * HEAD : BANK])
         finish(5, 1, 1)
+        add_and_store_late(3, k_flat[:, 2 * HEAD : BANK])

@@ -55,8 +55,7 @@ def tile_attention_pa_s_kernel(tc, x, w_qkv_words, w_qkv_scales, out_0, out_1, o
                 in_=w_qkv_scales[0, 4 * quadrant : 4 * quadrant + 4, :].bitcast(I32),
             )
         load_words(1, 2)
-        load_words(3, 1)
-        load_words(4, 2)
+        load_words(3, 3)
 
         warm = keep.tile([P, P], F32)
         nc.gpsimd.memset(warm[:], 0.0)
@@ -198,10 +197,15 @@ def tile_attention_pa_s_kernel(tc, x, w_qkv_words, w_qkv_scales, out_0, out_1, o
         def keep_clock_up():
             nc.tensor.matmul(warm_out[:], lhsT=warm[:], rhs=warm[:], start=True, stop=True)
 
-        def leave(target, n_heads, first_head, label):
-            result = keep.tile([P, HEAD * n_heads], F32, name="result_%s" % label)
-            nc.scalar.copy(out=result[:], in_=target[:, 0 : HEAD * n_heads])
-            nc.sync.dma_start(out=q_flat[:, HEAD * first_head : HEAD * (first_head + n_heads)], in_=result[:])
+        results = {}
+        for b in (0, 1, 2):
+            result = keep.tile([P, BANK], F32, name="result%d" % b)
+            results[b] = result
+
+        def store_q(b, first, after):
+            nc.sync.dma_start(
+                out=q_flat[:, BANK * b + HEAD * first : BANK * b + HEAD * after], in_=results[b][:, HEAD * first : HEAD * after]
+            )
 
         features_on_partitions(0, 0, 4)
         features_on_partitions(1, 0, 4)
@@ -251,9 +255,12 @@ def tile_attention_pa_s_kernel(tc, x, w_qkv_words, w_qkv_scales, out_0, out_1, o
                 op=ALU.mult,
             )
 
-        def add_and_store_late(i_late, dest):
+        def add_late(i_late):
             heads = slice(2 * i_late, 2 * i_late + 2)
             nc.vector.tensor_tensor(out=rotated_late[:, heads], in0=own[:, heads], in1=other[:, heads], op=ALU.add)
+
+        def store_late(first_piece, after_piece, dest):
+            heads = slice(2 * first_piece, 2 * after_piece)
             nc.sync.dma_start(out=dest, in_=rotated_late[:, heads].rearrange("p n c -> p (n c)"))
 
         targets = (1, 0, V_BANK)
@@ -261,23 +268,30 @@ def tile_attention_pa_s_kernel(tc, x, w_qkv_words, w_qkv_scales, out_0, out_1, o
         def finish(i_piece, b, half):
             target = banks[targets[i_piece % 3]][:, 0 : 2 * HEAD]
             turn_and_add(pairs[(b, half)], 2, target)
-            leave(target, 2, HEADS_PER_BANK * b + 2 * half, "%d_%d" % (b, half))
+            nc.scalar.copy(out=results[b][:, 2 * HEAD * half : 2 * HEAD * (half + 1)], in_=target)
 
         finish(0, 0, 0)
         finish(1, 0, 1)
+        store_q(0, 0, 4)
         keep_clock_up()
         finish(2, 2, 0)
         finish(3, 2, 1)
+        store_q(2, 0, 4)
         keep_clock_up()
         finish(4, 1, 0)
+        store_q(1, 0, 2)
         keep_clock_up()
         keep_clock_up()
         multiply_late(0, banks[3][:, 0 : 2 * HEAD])
         multiply_late(1, banks[3][:, 2 * HEAD : BANK])
         multiply_late(2, banks[K_BANK][:, 0 : 2 * HEAD])
         multiply_late(3, banks[K_BANK][:, 2 * HEAD : BANK])
-        add_and_store_late(0, q_flat[:, HEAD * 12 : HEAD * 14])
-        add_and_store_late(1, q_flat[:, HEAD * 14 : HEAD * 16])
-        add_and_store_late(2, k_flat[:, 0 : 2 * HEAD])
+        add_late(0)
+        add_late(1)
+        store_late(0, 2, q_flat[:, BANK * 3 : BANK * 4])
+        add_late(2)
+        store_late(2, 3, k_flat[:, 0 : 2 * HEAD])
         finish(5, 1, 1)
-        add_and_store_late(3, k_flat[:, 2 * HEAD : BANK])
+        store_q(1, 2, 4)
+        add_late(3)
+        store_late(3, 4, k_flat[:, 2 * HEAD : BANK])

@@ -227,71 +227,53 @@ def tile_attention_pa_s_kernel(tc, x, w_qkv_words, w_qkv_scales, out_0, out_1, o
         nc.sync.dma_start(out=out_2.rearrange("t n d -> t (n d)"), in_=v_sb[:])
 
         pairs = {}
-        for b, half in ((0, 0), (0, 1), (1, 0), (2, 0), (2, 1), (1, 1)):
-            if b == 1:
-                pairs[(b, half)] = multiply_by_tables(nc.gpsimd, heads_of(for_gpsimd[:], 2 * half, 2 * half + 2), 2, "g%d" % half)
-            else:
-                pairs[(b, half)] = multiply_by_tables(
-                    nc.vector, heads_of(banks[b][:], 2 * half, 2 * half + 2), 2, "u%d_%d" % (b, half)
-                )
+        pairs[(0, 0)] = multiply_by_tables(nc.vector, heads_of(banks[0][:], 0, 4), 4, "u0")
+        pairs[(1, 0)] = multiply_by_tables(nc.gpsimd, heads_of(for_gpsimd[:], 0, 2), 2, "g0")
+        pairs[(2, 0)] = multiply_by_tables(nc.vector, heads_of(banks[2][:], 0, 4), 4, "u2")
+        pairs[(1, 1)] = multiply_by_tables(nc.gpsimd, heads_of(for_gpsimd[:], 2, 4), 2, "g1")
 
-        LATE = 4
-        own = keep.tile([P, 2 * LATE, HEAD], F32)
-        other = keep.tile([P, 2 * LATE, HEAD], F32)
-        rotated_late = keep.tile([P, 2 * LATE, HEAD], F32)
+        LATE_HEADS = 2 * HEADS_PER_BANK
+        own = keep.tile([P, LATE_HEADS, HEAD], F32)
+        other = keep.tile([P, LATE_HEADS, HEAD], F32)
+        rotated_late = keep.tile([P, LATE_HEADS, HEAD], F32)
 
-        def multiply_late(i_late, source):
-            heads = slice(2 * i_late, 2 * i_late + 2)
+        def multiply_late(first, source):
+            heads = slice(first, first + HEADS_PER_BANK)
             nc.vector.tensor_tensor(
                 out=own[:, heads],
-                in0=source.rearrange("p (n c) -> p n c", n=2),
-                in1=by_token[:, 0, :].unsqueeze(1).to_broadcast([P, 2, HEAD]),
+                in0=source.rearrange("p (n c) -> p n c", n=HEADS_PER_BANK),
+                in1=by_token[:, 0, :].unsqueeze(1).to_broadcast([P, HEADS_PER_BANK, HEAD]),
                 op=ALU.mult,
             )
             nc.vector.tensor_tensor(
                 out=other[:, heads].rearrange("p n (i h) -> p n i h", h=2),
-                in0=source.rearrange("p (n i h) -> p n i h", n=2, h=2)[:, :, :, ::-1],
-                in1=by_token[:, 1, :].rearrange("p (i h) -> p i h", h=2).unsqueeze(1).to_broadcast([P, 2, PAIRS, 2]),
+                in0=source.rearrange("p (n i h) -> p n i h", n=HEADS_PER_BANK, h=2)[:, :, :, ::-1],
+                in1=by_token[:, 1, :].rearrange("p (i h) -> p i h", h=2).unsqueeze(1).to_broadcast([P, HEADS_PER_BANK, PAIRS, 2]),
                 op=ALU.mult,
             )
 
-        def add_late(i_late):
-            heads = slice(2 * i_late, 2 * i_late + 2)
+        def add_and_store_late(first, after, dest):
+            heads = slice(first, after)
             nc.vector.tensor_tensor(out=rotated_late[:, heads], in0=own[:, heads], in1=other[:, heads], op=ALU.add)
-
-        def store_late(first_piece, after_piece, dest):
-            heads = slice(2 * first_piece, 2 * after_piece)
             nc.sync.dma_start(out=dest, in_=rotated_late[:, heads].rearrange("p n c -> p (n c)"))
 
-        targets = (1, 0, V_BANK)
+        def finish(b, first, after, target_bank):
+            n_heads = after - first
+            target = banks[target_bank][:, 0 : HEAD * n_heads]
+            turn_and_add(pairs[(b, first // 2)], n_heads, target)
+            nc.scalar.copy(out=results[b][:, HEAD * first : HEAD * after], in_=target)
+            store_q(b, first, after)
 
-        def finish(i_piece, b, half):
-            target = banks[targets[i_piece % 3]][:, 0 : 2 * HEAD]
-            turn_and_add(pairs[(b, half)], 2, target)
-            nc.scalar.copy(out=results[b][:, 2 * HEAD * half : 2 * HEAD * (half + 1)], in_=target)
-
-        finish(0, 0, 0)
-        finish(1, 0, 1)
-        store_q(0, 0, 4)
+        finish(0, 0, 4, 1)
         keep_clock_up()
-        finish(2, 2, 0)
-        finish(3, 2, 1)
-        store_q(2, 0, 4)
+        finish(2, 0, 4, 0)
         keep_clock_up()
-        finish(4, 1, 0)
-        store_q(1, 0, 2)
+        finish(1, 0, 2, V_BANK)
         keep_clock_up()
         keep_clock_up()
-        multiply_late(0, banks[3][:, 0 : 2 * HEAD])
-        multiply_late(1, banks[3][:, 2 * HEAD : BANK])
-        multiply_late(2, banks[K_BANK][:, 0 : 2 * HEAD])
-        multiply_late(3, banks[K_BANK][:, 2 * HEAD : BANK])
-        add_late(0)
-        add_late(1)
-        store_late(0, 2, q_flat[:, BANK * 3 : BANK * 4])
-        add_late(2)
-        store_late(2, 3, k_flat[:, 0 : 2 * HEAD])
-        finish(5, 1, 1)
-        store_q(1, 2, 4)
-        add_late(3)
-        store_late(3, 4, k_flat[:, 2 * HEAD : BANK])
+        multiply_late(0, banks[3][:])
+        multiply_late(HEADS_PER_BANK, banks[K_BANK][:])
+        add_and_store_late(0, 4, q_flat[:, BANK * 3 : BANK * 4])
+        add_and_store_late(4, 6, k_flat[:, 0 : 2 * HEAD])
+        finish(1, 2, 4, 2)
+        add_and_store_late(6, 8, k_flat[:, 2 * HEAD : BANK])

import math

import concourse.mybir as mybir
from concourse.masks import make_identity

F32 = mybir.dt.float32
BF16 = mybir.dt.bfloat16
I32 = mybir.dt.int32
U32 = mybir.dt.uint32
U8 = mybir.dt.uint8
FP8X4 = mybir.dt.float8_e4m3fn_x4
FP4X4 = mybir.dt.float4_e2m1fn_x4
ALU = mybir.AluOpType
ACT = mybir.ActivationFunctionType

P = 128
DIM = 512
HEAD = 128
PAIRS = HEAD // 2
Q_HEADS, KV_HEADS = 16, 4
N_ALL = (Q_HEADS + 2 * KV_HEADS) * HEAD
BANK = 512
HEADS_PER_BANK = BANK // HEAD
ROPE_BANKS = (Q_HEADS + KV_HEADS) // HEADS_PER_BANK
THETA = 10000.0
TWO_PI = 2.0 * math.pi
WARM_MATMULS = 3
BRIDGE_MATMULS = 2
V_BANK = ROPE_BANKS
K_BANK = ROPE_BANKS - 1

FLOPS = 2 * P * DIM * N_ALL


def tile_attention_pa_s_kernel(tc, x, w_qkv_words, w_qkv_scales, out_0, out_1, out_2):
    nc = tc.nc
    with tc.tile_pool(name="keep", bufs=1) as keep, tc.psum_pool(name="psum", bufs=1) as psum, tc.manual_schedule():
        x_sb = keep.tile([P, DIM], BF16)
        nc.sync.dma_start(out=x_sb[:], in_=x)

        w_words = keep.tile([P, 2 * N_ALL], U8, align_bytes=64)

        def load_words(first_bank, n_banks):
            cols = slice(2 * BANK * first_bank, 2 * BANK * (first_bank + n_banks))
            nc.sync.dma_start(out=w_words[:, cols].bitcast(I32), in_=w_qkv_words[0, :, cols].bitcast(I32))

        w_scales = keep.tile([P, N_ALL], U8, align_bytes=64)
        steps = keep.tile([P, HEAD], F32)
        nc.vector.memset(w_scales[:].bitcast(I32), 0)

        load_words(0, 1)
        for quadrant in range(4):
            nc.sync.dma_start(
                out=w_scales[32 * quadrant : 32 * quadrant + 4, :].bitcast(I32),
                in_=w_qkv_scales[0, 4 * quadrant : 4 * quadrant + 4, :].bitcast(I32),
            )
        load_words(1, 2)
        load_words(3, 3)

        warm = keep.tile([P, P], F32)
        nc.gpsimd.memset(warm[:], 0.0)
        ratio = THETA ** (-1.0 / PAIRS)
        nc.gpsimd.memset(steps[:], -1.0)
        nc.gpsimd.tensor_scalar(
            out=steps[:, 0:HEAD:2], in0=steps[:, 1:HEAD:2], scalar1=ratio, scalar2=0.0, op0=ALU.mult, op1=ALU.add
        )
        ident = keep.tile([P, P], F32)
        make_identity(nc, ident[:])
        token = keep.tile([P, P], F32)
        nc.gpsimd.iota(token[:], pattern=[[1, P]], base=0, channel_multiplier=0, allow_small_or_imprecise_dtypes=True)
        swap = keep.tile([P, P], F32)
        ident_pairs = ident[:].rearrange("p (i h) -> p i h", h=2)
        swap_pairs = swap[:].rearrange("p (i h) -> p i h", h=2)
        nc.gpsimd.tensor_copy(out=swap_pairs[:, :, 0], in_=ident_pairs[:, :, 1])
        nc.gpsimd.tensor_copy(out=swap_pairs[:, :, 1], in_=ident_pairs[:, :, 0])

        sin_first = keep.tile([P, 1], F32)
        nc.scalar.activation(out=sin_first[:], in_=warm[:, 0:1], func=ACT.Sin)

        signed_row = keep.tile([P, HEAD], F32)
        nc.vector.tensor_tensor_scan(
            out=signed_row[:],
            data0=steps[:],
            data1=warm[:, 0:1].to_broadcast([P, HEAD]),
            initial=-1.0 / (TWO_PI * ratio),
            op0=ALU.mult,
            op1=ALU.add,
        )
        shift = keep.tile([P, 2], F32)
        nc.vector.memset(shift[:, 0:1], 0.25)
        nc.vector.memset(shift[:, 1:2], 0.0)

        picked = keep.tile([P, HEAD], F32)
        signed_col = keep.tile([P, 1], F32)
        nc.vector.scalar_tensor_tensor(
            out=picked[:],
            in0=ident[:],
            scalar=1.0,
            in1=signed_row[:],
            op0=ALU.mult,
            op1=ALU.mult,
            accum_out=signed_col[:],
        )
        turns = keep.tile([P, 2, P], F32)
        whole = keep.tile([P, 2, P], I32)
        for rounded_or_not in (turns, whole):
            nc.vector.scalar_tensor_tensor(
                out=rounded_or_not[:],
                in0=token[:].unsqueeze(1).to_broadcast([P, 2, P]),
                scalar=signed_col[:, 0:1],
                in1=shift[:].unsqueeze(2).to_broadcast([P, 2, P]),
                op0=ALU.mult,
                op1=ALU.add,
            )
        left = keep.tile([P, 2, P], F32)
        nc.vector.tensor_tensor(out=left[:], in0=turns[:], in1=whole[:], op=ALU.subtract)

        warm_out = psum.tile([P, P], F32)
        for i_warm in range(WARM_MATMULS):
            nc.tensor.matmul(warm_out[:], lhsT=warm[:], rhs=warm[:], start=True, stop=True)

        x_words = x_sb[:].bitcast(F32)
        x_t = psum.tile([P, 2, P], F32)
        for u in range(2):
            nc.tensor.transpose(x_t[:, u, :], x_words[:, u : DIM // 2 : 2], ident[:])
        for i_warm in range(BRIDGE_MATMULS):
            nc.tensor.matmul(warm_out[:], lhsT=warm[:], rhs=warm[:], start=True, stop=True)
        x_grouped = keep.tile([P, 4 * P], BF16, align_bytes=64)
        nc.scalar.copy(
            out=x_grouped[:].bitcast(F32).rearrange("p (t u) -> p t u", u=2),
            in_=x_t[:].rearrange("p u t -> p t u"),
        )
        x_codes = keep.tile([P, P], U32, align_bytes=64)
        x_scales = keep.tile([P, P], U8, align_bytes=64)
        nc.vector.quantize_mx(out=x_codes[:].bitcast(FP8X4), scales=x_scales[:], in_=x_grouped[:])

        tables = keep.tile([P, 2, P], F32)
        nc.scalar.activation(out=tables[:], in_=left[:], func=ACT.Sin, scale=TWO_PI)

        banks = []
        for b in range(ROPE_BANKS + 1):
            acc = psum.tile([P, BANK], F32, name="acc%d" % b)
            banks.append(acc)

        def features_on_partitions(b, first, after):
            for n in range(first, after):
                head = HEADS_PER_BANK * b + n
                nc.tensor.matmul_mx(
                    out=banks[b][:, HEAD * n : HEAD * (n + 1)],
                    lhsT=w_words[:, 2 * HEAD * head : 2 * HEAD * (head + 1)].bitcast(FP4X4),
                    lhsT_scale=w_scales[:, HEAD * head : HEAD * (head + 1)],
                    rhs=x_codes[:].bitcast(FP8X4),
                    rhs_scale=x_scales[:],
                    start=True,
                    stop=True,
                )

        def tokens_on_partitions(b, first, after):
            head = HEADS_PER_BANK * b + first
            n_heads = after - first
            nc.tensor.matmul_mx(
                out=banks[b][:, HEAD * first : HEAD * after],
                lhsT=x_codes[:].bitcast(FP8X4),
                lhsT_scale=x_scales[:],
                rhs=w_words[:, 2 * HEAD * head : 2 * HEAD * (head + n_heads)].bitcast(FP4X4),
                rhs_scale=w_scales[:, HEAD * head : HEAD * (head + n_heads)],
                start=True,
                stop=True,
            )

        q_flat = out_0.rearrange("t n d -> t (n d)")
        k_flat = out_1.rearrange("t n d -> t (n d)")

        def heads_of(flat, first, after):
            return flat[:, HEAD * first : HEAD * after].rearrange("p (n c) -> p n c", c=HEAD)

        def multiply_by_tables(engine, source, n_heads, label):
            pair = []
            for which in range(2):
                product = keep.tile([P, n_heads, P], F32, name="product_%s_%d" % (label, which))
                engine.tensor_tensor(
                    out=product[:],
                    in0=source,
                    in1=tables[:, which, :].unsqueeze(1).to_broadcast([P, n_heads, P]),
                    op=ALU.mult,
                )
                pair.append(product)
            return pair

        def turn_and_add(pair, n_heads, target):
            with_cos, with_sin = pair
            for n in range(n_heads):
                rotated = target[:, HEAD * n : HEAD * (n + 1)]
                nc.tensor.matmul(rotated, lhsT=with_cos[:, n, :], rhs=ident[:], is_transpose=True, start=True, stop=False)
                nc.tensor.matmul(rotated, lhsT=with_sin[:, n, :], rhs=swap[:], is_transpose=True, start=False, stop=True)

        def keep_clock_up():
            nc.tensor.matmul(warm_out[:], lhsT=warm[:], rhs=warm[:], start=True, stop=True)

        results = {}
        for b in (0, 1, 2):
            result = keep.tile([P, BANK], F32, name="result%d" % b)
            results[b] = result

        def store_q(b, first, after):
            nc.sync.dma_start(
                out=q_flat[:, BANK * b + HEAD * first : BANK * b + HEAD * after], in_=results[b][:, HEAD * first : HEAD * after]
            )

        features_on_partitions(0, 0, 4)
        features_on_partitions(1, 0, 4)
        features_on_partitions(2, 0, 4)
        tables_turned = x_t
        nc.tensor.transpose(tables_turned[:, 0, :], tables[:, 0, :], ident[:])
        nc.tensor.transpose(tables_turned[:, 1, :], tables[:, 1, :], swap[:])
        tokens_on_partitions(3, 0, 4)
        tokens_on_partitions(V_BANK, 0, 4)
        tokens_on_partitions(K_BANK, 0, 4)

        for_gpsimd = keep.tile([P, BANK], F32)
        nc.scalar.copy(out=for_gpsimd[:, 0 : 2 * HEAD], in_=banks[1][:, 0 : 2 * HEAD])
        nc.scalar.copy(out=for_gpsimd[:, 2 * HEAD : BANK], in_=banks[1][:, 2 * HEAD : BANK])
        by_token = keep.tile([P, 2, P], F32)
        nc.scalar.copy(out=by_token[:], in_=tables_turned[:])
        v_sb = keep.tile([P, BANK], F32)
        nc.scalar.copy(out=v_sb[:], in_=banks[V_BANK][:])
        nc.sync.dma_start(out=out_2.rearrange("t n d -> t (n d)"), in_=v_sb[:])

        pairs = {}
        pairs[(0, 0)] = multiply_by_tables(nc.vector, heads_of(banks[0][:], 0, 4), 4, "u0")
        pairs[(1, 0)] = multiply_by_tables(nc.gpsimd, heads_of(for_gpsimd[:], 0, 2), 2, "g0")
        pairs[(2, 0)] = multiply_by_tables(nc.vector, heads_of(banks[2][:], 0, 4), 4, "u2")
        pairs[(1, 1)] = multiply_by_tables(nc.gpsimd, heads_of(for_gpsimd[:], 2, 4), 2, "g1")

        LATE_HEADS = 2 * HEADS_PER_BANK
        own = keep.tile([P, LATE_HEADS, HEAD], F32)
        other = keep.tile([P, LATE_HEADS, HEAD], F32)
        rotated_late = keep.tile([P, LATE_HEADS, HEAD], F32)

        def multiply_late(first, source):
            heads = slice(first, first + HEADS_PER_BANK)
            nc.vector.tensor_tensor(
                out=own[:, heads],
                in0=source.rearrange("p (n c) -> p n c", n=HEADS_PER_BANK),
                in1=by_token[:, 0, :].unsqueeze(1).to_broadcast([P, HEADS_PER_BANK, HEAD]),
                op=ALU.mult,
            )
            nc.vector.tensor_tensor(
                out=other[:, heads].rearrange("p n (i h) -> p n i h", h=2),
                in0=source.rearrange("p (n i h) -> p n i h", n=HEADS_PER_BANK, h=2)[:, :, :, ::-1],
                in1=by_token[:, 1, :].rearrange("p (i h) -> p i h", h=2).unsqueeze(1).to_broadcast([P, HEADS_PER_BANK, PAIRS, 2]),
                op=ALU.mult,
            )

        def add_and_store_late(first, after, dest):
            heads = slice(first, after)
            nc.vector.tensor_tensor(out=rotated_late[:, heads], in0=own[:, heads], in1=other[:, heads], op=ALU.add)
            nc.sync.dma_start(out=dest, in_=rotated_late[:, heads].rearrange("p n c -> p (n c)"))

        def finish(b, first, after, target_bank):
            n_heads = after - first
            target = banks[target_bank][:, 0 : HEAD * n_heads]
            turn_and_add(pairs[(b, first // 2)], n_heads, target)
            nc.scalar.copy(out=results[b][:, HEAD * first : HEAD * after], in_=target)
            store_q(b, first, after)

        finish(0, 0, 4, 1)
        keep_clock_up()
        finish(2, 0, 4, 0)
        keep_clock_up()
        finish(1, 0, 2, V_BANK)
        keep_clock_up()
        keep_clock_up()
        multiply_late(0, banks[3][:])
        multiply_late(HEADS_PER_BANK, banks[K_BANK][:])
        add_and_store_late(0, 4, q_flat[:, BANK * 3 : BANK * 4])
        add_and_store_late(4, 6, k_flat[:, 0 : 2 * HEAD])
        finish(1, 2, 4, 2)
        add_and_store_late(6, 8, k_flat[:, 2 * HEAD : BANK])
